import numpy as np
import ml_dtypes


def mxq(x, axis, fmt="e4m3"):
    dtype, down = {"e4m3": (ml_dtypes.float8_e4m3fn, 7), "e5m2": (ml_dtypes.float8_e5m2, 14)}[fmt]
    v = np.moveaxis(np.asarray(x, np.float32).astype(ml_dtypes.bfloat16).astype(np.float64), axis, -1)
    blocks = v.reshape(v.shape[:-1] + (-1, 32))
    amax = np.abs(blocks).max(-1, keepdims=True)
    byte = np.maximum(np.where(amax > 0, np.frexp(amax)[1] - 1 + 127, 0) - down, 1)
    scale = np.exp2(byte - 127.0)
    codes = (blocks / scale).astype(np.float32).astype(dtype).astype(np.float64)
    return np.moveaxis((codes * scale).reshape(v.shape), -1, axis)


WIDE = False


def mx_kscale(k):
    if not WIDE:
        return np.ones(k)
    levels = np.array([10, -10, 5, -5, 0])
    a = np.random.permutation(np.resize(levels, k // 512 * 4)).reshape(k // 512, 4)
    idx = np.arange(k)
    return np.exp2(a[idx // 512, idx % 128 // 32])


BF16 = ml_dtypes.bfloat16


def bf(x):
    return np.asarray(x, np.float32).astype(BF16)


def f64(x):
    return np.asarray(x).astype(np.float64)


E2M1 = np.array([0.0, 0.5, 1.0, 1.5, 2.0, 3.0, 4.0, 6.0, -0.0, -0.5, -1.0, -1.5, -2.0, -3.0, -4.0, -6.0])


def pack_weight(w, fmt):
    k, n = w.shape
    w = f64(bf(w)).reshape(k // 32, 32, n)
    amax = np.abs(w).max(1)
    if fmt == "e4m3":
        byte = np.frexp(amax)[1] - 1 + 127 - 7
    else:
        mant, ex = np.frexp(amax / 6.0)
        byte = np.where(mant > 0.5, ex, ex - 1) + 127
    byte = np.clip(np.where(amax > 0, byte, 1), 1, 254)
    scaled = (w * np.exp2(127.0 - byte)[:, None, :]).reshape(k, n).astype(np.float32)
    by_word = np.ascontiguousarray(scaled.reshape(k // 512, 128, 4, n).transpose(0, 1, 3, 2))
    if fmt == "e4m3":
        words = by_word.astype(ml_dtypes.float8_e4m3fn).view(np.uint8)
    else:
        c = by_word.astype(ml_dtypes.float4_e2m1fn).view(np.uint8) & 0xF
        words = c[..., 0::2] | (c[..., 1::2] << 4)
    return np.ascontiguousarray(words), np.ascontiguousarray(byte.astype(np.uint8).reshape(k // 512, 16, n))


def unpack_weight(words, scales, fmt):
    g, p, n, _ = words.shape
    if fmt == "e4m3":
        vals = np.ascontiguousarray(words).view(ml_dtypes.float8_e4m3fn).astype(np.float64)
    else:
        nib = np.empty((g, p, n, 4), np.uint8)
        nib[..., 0::2] = words & 0xF
        nib[..., 1::2] = words >> 4
        vals = E2M1[nib]
    vals = vals * np.repeat(np.exp2(scales.astype(np.float64) - 127.0), 8, axis=1)[..., None]
    return vals.transpose(0, 1, 3, 2).reshape(g * 512, n)


B, C, H, W, P, DIM = 8, 8, 128, 128, 16, 768
SHIFT = P // 2
WD = 5 * C * P * P // 4
N = (H // P) * (W // P)
EPS = 1e-5
XS = 0.015
FMT = "e4m3"


def patch_shift(x, shift):
    xp = np.pad(x, ((0, 0), (0, 0), (shift, shift), (shift, shift)))
    s2 = 2 * shift
    return np.concatenate([x, xp[:, :, :-s2, :-s2], xp[:, :, :-s2, s2:], xp[:, :, s2:, :-s2], xp[:, :, s2:, s2:]], axis=1)


def haar_detail_mean(x):
    b_, c_, h, w = x.shape
    r = x.reshape(b_, c_, h // 2, 2, w // 2, 2)
    return (3.0 * r[:, :, :, 0, :, 0] - r[:, :, :, 0, :, 1] - r[:, :, :, 1, :, 0] - r[:, :, :, 1, :, 1]) / 6.0


def patchify(x, p):
    b_, c_, hh, ww = x.shape
    h, w = hh // p, ww // p
    return x.reshape(b_, c_, h, p, w, p).transpose(0, 2, 4, 3, 5, 1).reshape(b_, h * w, p * p * c_)


def layernorm(u, g, b):
    m = u.mean(-1, keepdims=True)
    v = np.square(u - m).mean(-1, keepdims=True)
    return (u - m) / np.sqrt(v + EPS) * g + b


def setup_inputs():
    s = mx_kscale(WD)
    x = bf(np.random.standard_normal((B, C, H, W)) * XS)
    ln2_g = bf((1.0 + 0.1 * np.random.standard_normal(WD)) * s)
    ln2_b = bf(0.1 * np.random.standard_normal(WD) * s)
    w2_words, w2_scales = pack_weight(np.random.standard_normal((WD, DIM)) / np.sqrt(WD) / s[:, None], FMT)
    b2 = bf(0.3 * np.random.standard_normal(DIM))
    tok = bf(np.random.standard_normal((B, N, DIM)))
    return {"x": x,
            "ln2_g": ln2_g,
            "ln2_b": ln2_b,
            "w2_words": w2_words,
            "w2_scales": w2_scales,
            "b2": b2,
            "tok": tok}


def reference(x, ln2_g, ln2_b, w2_words, w2_scales, b2, tok):
    waves = haar_detail_mean(patch_shift(f64(x), SHIFT))
    z = layernorm(patchify(waves, P // 2), f64(ln2_g), f64(ln2_b))
    wtok = (mxq(z, 2, "e4m3") @ unpack_weight(w2_words, w2_scales, FMT)) + f64(b2)
    return f64(tok) + wtok

@@ -1,0 +1,293 @@
+import concourse.mybir as mybir
+from concourse.masks import make_identity
+
+F32 = mybir.dt.float32
+BF16 = mybir.dt.bfloat16
+I32 = mybir.dt.int32
+U32 = mybir.dt.uint32
+U8 = mybir.dt.uint8
+FP8X4 = mybir.dt.float8_e4m3fn_x4
+ALU = mybir.AluOpType
+ACT = mybir.ActivationFunctionType
+AXIS = mybir.AxisListType
+
+P = 128
+CHANNELS = 8
+TOKENS = 512
+TOKEN_TILES = TOKENS // P
+K = 2560
+PACK = 4
+PASSES = K // (P * PACK)
+DIM = 768
+N_CUTS = ((0, 512), (512, 768))
+PAD = 72
+PLANE = PAD + TOKENS + PAD
+EPS_36 = 36.0 * 1e-5
+
+FLOPS = 2 * TOKENS * K * DIM
+
+
+def scale_and_shift(nc, m, out, in_, scale, shift):
+    if m % 2 == 0:
+        nc.scalar.activation(out=out, in_=in_, func=ACT.Identity, bias=shift, scale=scale)
+    else:
+        nc.vector.tensor_scalar(out=out, in0=in_, scalar1=scale, scalar2=shift, op0=ALU.mult, op1=ALU.add)
+
+
+def tile_shiftedpatchtokenization_pb_kernel(tc, x, ln2_g, ln2_b, w2_words, w2_scales, b2, tok, out):
+    nc = tc.nc
+    with tc.tile_pool(name="keep", bufs=1) as keep, tc.tile_pool(name="work", bufs=2) as work, tc.psum_pool(
+        name="psum", bufs=8
+    ) as psum:
+        x_sb = keep.tile([P, CHANNELS, 1024], BF16)
+        for ch in range(CHANNELS):
+            nc.sync.dma_start(out=x_sb[:, ch, :], in_=x[:, ch].rearrange("b (iy r) w -> iy b (r w)", r=8))
+
+        gain_bf = keep.tile([P, PASSES, PACK], BF16)
+        offs_bf = keep.tile([P, PASSES, PACK], BF16)
+        nc.sync.dma_start(out=gain_bf[:], in_=ln2_g.rearrange("(g p t) -> p g t", g=PASSES, p=P))
+        nc.sync.dma_start(out=offs_bf[:], in_=ln2_b.rearrange("(g p t) -> p g t", g=PASSES, p=P))
+
+        w_scales = keep.tile([P, PASSES, DIM], U8, align_bytes=64)
+        nc.vector.memset(w_scales[:].bitcast(I32), 0)
+        for quad in range(4):
+            nc.sync.dma_start(
+                out=w_scales[32 * quad : 32 * quad + 4].bitcast(I32),
+                in_=w2_scales[:, 4 * quad : 4 * quad + 4, :].rearrange("g r n -> r g n").bitcast(I32),
+            )
+        w_words = keep.tile([P, PASSES, DIM], U32, align_bytes=64)
+        nc.sync.dma_start(
+            out=w_words[:].bitcast(I32), in_=w2_words.rearrange("g p n t -> p g (n t)").bitcast(I32)
+        )
+        tok_bf = keep.tile([P, TOKEN_TILES, DIM], BF16)
+        nc.sync.dma_start(out=tok_bf[:], in_=tok.flatten_outer_dims().rearrange("(m p) n -> p m n", p=P))
+        b2_bf = keep.tile([P, DIM], BF16)
+        nc.sync.dma_start(out=b2_bf[:], in_=b2.partition_broadcast(P))
+
+        one = keep.tile([P, 1], F32)
+        nc.vector.memset(one[:], 1.0)
+        nc.scalar.activation(out=one[:], in_=one[:], func=ACT.Sqrt)
+
+        ident = keep.tile([P, P], F32)
+        make_identity(nc, ident[:])
+
+        sort_ch = keep.tile([P, P], F32)
+        sort_view = sort_ch[:].rearrange("p (th r chh tl) -> p th r chh tl", th=2, r=16, chh=2, tl=2)
+        ident_view = ident[:].rearrange("p (chh th tl r) -> p th r chh tl", chh=2, th=2, tl=2, r=16)
+        for th in range(2):
+            nc.vector.tensor_copy(out=sort_view[:, th], in_=ident_view[:, th])
+
+        WIDE, NEAR = 0, 1
+        pick_rows = keep.tile([P, 2, 2, 2, 8, 8], F32)
+        nc.vector.memset(pick_rows[:], 0.0)
+        by_row = ident[:].rearrange("p (i py b) -> p i py b", i=8, py=2, b=8)
+        near = pick_rows[:, NEAR, 0, 0]
+        wide = pick_rows[:, WIDE, 0, 0]
+        nc.vector.tensor_tensor(out=near, in0=by_row[:, :, 0, :], in1=by_row[:, :, 1, :], op=ALU.add)
+        nc.vector.tensor_copy(out=wide, in_=near)
+        nc.vector.tensor_tensor(out=wide[:, 1:8], in0=wide[:, 1:8], in1=by_row[:, 0:7, 1, :], op=ALU.add)
+        nc.vector.tensor_tensor(out=wide[:, 0:7], in0=wide[:, 0:7], in1=by_row[:, 1:8, 0, :], op=ALU.add)
+        nc.vector.tensor_copy(out=pick_rows[:, NEAR, 1, 1], in_=near)
+        nc.vector.tensor_copy(out=pick_rows[:, WIDE, 1, 1], in_=wide)
+
+        by_token = ident[:].rearrange("p (jlo i b) -> p jlo i b", jlo=2, i=8, b=8)
+        at_edge = keep.tile([P, 2], F32)
+        nc.vector.tensor_reduce(out=at_edge[:, 0:1], in_=by_token[:, :, 0, :], axis=AXIS.XY, op=ALU.add)
+        nc.vector.tensor_reduce(out=at_edge[:, 1:2], in_=by_token[:, :, 7, :], axis=AXIS.XY, op=ALU.add)
+        inside = keep.tile([P, 2], F32)
+        nc.vector.tensor_scalar(out=inside[:], in0=at_edge[:], scalar1=-1.0, scalar2=1.0, op0=ALU.mult, op1=ALU.add)
+
+        gain = keep.tile([P, PASSES, PACK], F32)
+        offs = keep.tile([P, PASSES, PACK], F32)
+        nc.vector.tensor_copy(out=gain[:], in_=gain_bf[:])
+        nc.vector.tensor_copy(out=offs[:], in_=offs_bf[:])
+
+        cells = keep.tile([P, 2, 2, PLANE], F32)
+        nc.vector.memset(cells[:, :, :, 0:PAD], 0.0)
+        nc.vector.memset(cells[:, :, :, PAD + TOKENS : PLANE], 0.0)
+
+        cell_sum = keep.tile([P, 18], F32)
+        cell_sq = keep.tile([P, 18], F32)
+        nc.vector.memset(cell_sum[:], 0.0)
+        nc.vector.memset(cell_sq[:], 0.0)
+
+        tok_b2 = keep.tile([P, TOKEN_TILES, DIM], F32)
+        for m in range(TOKEN_TILES):
+            nc.gpsimd.tensor_tensor(out=tok_b2[:, m, :], in0=tok_bf[:, m, :], in1=b2_bf[:], op=ALU.add)
+
+        hw = keep.tile([P, 16, CHANNELS, 16], F32)
+        for ch in range(CHANNELS):
+            blocks = x_sb[:, ch, :].rearrange("p (yy ry c rx) -> p yy ry c rx", yy=4, ry=2, c=64, rx=2)
+            upper = work.tile([P, 4, 64], F32)
+            lower = work.tile([P, 4, 64], F32)
+            nc.vector.scalar_tensor_tensor(
+                out=upper[:], in0=blocks[:, :, 0, :, 0], scalar=3.0, in1=blocks[:, :, 0, :, 1],
+                op0=ALU.mult, op1=ALU.subtract,
+            )
+            nc.vector.tensor_tensor(out=lower[:], in0=blocks[:, :, 1, :, 0], in1=blocks[:, :, 1, :, 1], op=ALU.add)
+            nc.vector.tensor_tensor(
+                out=hw[:, :, ch, :].rearrange("p X (yy xx) -> p X yy xx", yy=4),
+                in0=upper[:].rearrange("p yy (X xx) -> p X yy xx", xx=4),
+                in1=lower[:].rearrange("p yy (X xx) -> p X yy xx", xx=4),
+                op=ALU.subtract,
+            )
+
+        nc.vector.tensor_reduce(
+            out=cell_sum[:, 1:17], in_=hw[:].rearrange("p X ch r -> p X (ch r)"), axis=AXIS.X, op=ALU.add
+        )
+        squares = keep.tile([P, 16, P], F32)
+        for X in range(16):
+            nc.scalar.activation(
+                out=squares[:, X, :], in_=hw[:, X].rearrange("p ch r -> p (ch r)"), func=ACT.Square,
+                accum_out=cell_sq[:, 1 + X : 2 + X],
+            )
+        row_sums = keep.tile([P, 2, 2, 2, TOKEN_TILES], F32)
+        for stat, per_cell in enumerate((cell_sum, cell_sq)):
+            straddling = work.tile([P, 9], F32)
+            pairs = per_cell[:].rearrange("p (J two) -> p J two", two=2)
+            nc.vector.tensor_tensor(out=straddling[:], in0=pairs[:, :, 0], in1=pairs[:, :, 1], op=ALU.add)
+            nc.vector.tensor_tensor(
+                out=row_sums[:, WIDE, :, stat, :].rearrange("p jlo m -> p m jlo"),
+                in0=straddling[:, 0:8].rearrange("p (m jlo) -> p m jlo", jlo=2),
+                in1=straddling[:, 1:9].rearrange("p (m jlo) -> p m jlo", jlo=2),
+                op=ALU.add,
+            )
+            own = per_cell[:, 1:17].rearrange("p (m jlo two) -> p m jlo two", jlo=2, two=2)
+            nc.vector.tensor_tensor(
+                out=row_sums[:, NEAR, :, stat, :].rearrange("p jlo m -> p m jlo"),
+                in0=own[:, :, :, 0], in1=own[:, :, :, 1], op=ALU.add,
+            )
+        totals = psum.tile([P, 512], F32, tag="bank")
+        for step, (kind, jlo) in enumerate(((WIDE, 0), (WIDE, 1), (NEAR, 0), (NEAR, 1))):
+            nc.tensor.matmul(
+                out=totals[:, 0:8],
+                lhsT=pick_rows[:, kind, jlo].rearrange("p a i b -> p (a i b)"),
+                rhs=row_sums[:, kind, jlo].rearrange("p s m -> p (s m)"),
+                start=(step == 0), stop=(step == 3),
+            )
+        mean = keep.tile([P, TOKEN_TILES], F32)
+        spread = keep.tile([P, TOKEN_TILES], F32)
+        mean_sq = keep.tile([P, TOKEN_TILES], F32)
+        nc.vector.tensor_scalar(out=mean[:], in0=totals[:, 0:4], scalar1=1.0 / K, scalar2=None, op0=ALU.mult)
+        nc.vector.tensor_scalar(
+            out=spread[:], in0=totals[:, 4:8], scalar1=1.0 / K, scalar2=EPS_36, op0=ALU.mult, op1=ALU.add
+        )
+        nc.vector.tensor_tensor(out=mean_sq[:], in0=mean[:], in1=mean[:], op=ALU.mult)
+        nc.vector.tensor_tensor(out=spread[:], in0=spread[:], in1=mean_sq[:], op=ALU.subtract)
+        nc.scalar.activation(out=spread[:], in_=spread[:], func=ACT.Sqrt)
+        rstd = keep.tile([P, 3, TOKEN_TILES], F32)
+        shift = keep.tile([P, TOKEN_TILES], F32)
+        nc.vector.reciprocal(out=rstd[:, 0, :], in_=spread[:])
+        nc.vector.scalar_tensor_tensor(
+            out=shift[:], in0=mean[:], scalar=-1.0, in1=rstd[:, 0, :], op0=ALU.mult, op1=ALU.mult
+        )
+        for edge in range(2):
+            nc.vector.tensor_scalar(
+                out=rstd[:, 1 + edge, :], in0=rstd[:, 0, :], scalar1=inside[:, edge : edge + 1], scalar2=None,
+                op0=ALU.mult,
+            )
+
+        for px in range(2):
+            for jh in range(2):
+                bank = psum.tile([P, 512], F32, tag="bank")
+                for jl in range(4):
+                    nc.tensor.transpose(
+                        out=bank[:, P * jl : P * jl + P],
+                        in_=hw[:, 2 * (4 * jh + jl) + px].rearrange("p ch r -> p (ch r)"),
+                        identity=ident[:],
+                    )
+                by_py = bank[:].rearrange("p (jl i py b) -> p py jl i b", jl=4, i=8, py=2, b=8)
+                for py in range(2):
+                    to = cells[:, py, px, PAD + 256 * jh : PAD + 256 * jh + 256].rearrange(
+                        "p (jl i b) -> p jl i b", jl=4, i=8
+                    )
+                    if jh == 0:
+                        nc.scalar.copy(out=to, in_=by_py[:, py])
+                    else:
+                        nc.vector.tensor_copy(out=to, in_=by_py[:, py])
+
+        y = []
+        for m in range(TOKEN_TILES):
+            y_m = keep.tile([P, 2, 64, 20], F32, name="y%d" % m)
+            y.append(y_m)
+            first = PAD + P * m
+            bank = psum.tile([P, 512], F32, tag="bank")
+            quarters = bank[:].rearrange("p (th qy yy qx r) -> p th qy yy qx r", th=2, qy=2, yy=4, qx=2, r=16)
+            for qy in range(2):
+                for qx in range(2):
+                    nc.tensor.transpose(
+                        out=quarters[:, :, qy, :, qx, :], in_=cells[:, qy, qx, first : first + P], identity=sort_ch[:]
+                    )
+            scale_and_shift(
+                nc, m, y_m[:, :, :, 0:4], bank[:].rearrange("p (th pix e) -> p th pix e", th=2, e=4),
+                rstd[:, 0, m : m + 1], shift[:, m : m + 1],
+            )
+            for qy in range(2):
+                for down in range(2):
+                    oy = qy - 1 + 2 * down
+                    py, di = oy % 2, oy // 2
+                    bank = psum.tile([P, 512], F32, tag="bank")
+                    quarters = bank[:].rearrange(
+                        "p (a qx xx right e) -> p a qx xx right e", a=8, qx=2, xx=4, right=2, e=4
+                    )
+                    for qx in range(2):
+                        for right in range(2):
+                            ox = qx - 1 + 2 * right
+                            px, dj = ox % 2, ox // 2
+                            start = first + 64 * dj + 8 * di
+                            nc.tensor.transpose(
+                                out=quarters[:, :, qx, :, right, :], in_=cells[:, py, px, start : start + P],
+                                identity=sort_ch[:],
+                            )
+                    which = {-1: 1, 0: 0, 1: 2}[di]
+                    scale_and_shift(
+                        nc, m, y_m[:, :, 32 * qy : 32 * qy + 32, 4 + 8 * down : 12 + 8 * down],
+                        bank[:].rearrange("p (th pix e) -> p th pix e", th=2, e=8),
+                        rstd[:, which, m : m + 1], shift[:, m : m + 1],
+                    )
+
+        z_words = keep.tile([P, PASSES, TOKENS], U32, align_bytes=64)
+        z_scales = keep.tile([P, PASSES, TOKENS], U8, align_bytes=64)
+        for g in range(PASSES):
+            z_planes = work.tile([P, PACK, TOKENS], BF16)
+            for t in range(PACK):
+                th, tl = t // 2, t % 2
+                bank = psum.tile([P, 512], F32, tag="bank")
+                for m in range(TOKEN_TILES):
+                    half = y[m][:, th].rearrange("p pix e -> p (pix e)")
+                    nc.tensor.transpose(
+                        out=bank[:, P * m : P * m + P], in_=half[:, 256 * g + tl : 256 * g + 256 : 2],
+                        identity=ident[:],
+                    )
+                nc.scalar.activation(
+                    out=z_planes[:, t, :].rearrange("p (b i j) -> p b i j", b=8, i=8),
+                    in_=bank[:].rearrange("p (j i b) -> p b i j", j=8, i=8),
+                    func=ACT.Identity, bias=offs[:, g, t : t + 1], scale=gain[:, g, t : t + 1],
+                )
+            z_grouped = work.tile([P, TOKENS, PACK], BF16, align_bytes=64)
+            nc.vector.tensor_copy(
+                out=z_grouped[:].rearrange("p (c i) t -> p c t i", i=4),
+                in_=z_planes[:].rearrange("p t (c i) -> p c t i", i=4),
+            )
+            nc.vector.quantize_mx(
+                out=z_words[:, g, :].bitcast(FP8X4), scales=z_scales[:, g, :],
+                in_=z_grouped[:].rearrange("p n t -> p (n t)"),
+            )
+
+        out_rows = out.flatten_outer_dims()
+        for m in range(TOKEN_TILES):
+            rows = slice(P * m, P * m + P)
+            result = work.tile([P, DIM], F32)
+            for lo, hi in N_CUTS:
+                acc = psum.tile([P, 512], F32, tag="bank")
+                for g in range(PASSES):
+                    nc.tensor.matmul_mx(
+                        out=acc[:, 0 : hi - lo],
+                        lhsT=z_words[:, g, rows].bitcast(FP8X4), lhsT_scale=z_scales[:, g, rows],
+                        rhs=w_words[:, g, lo:hi].bitcast(FP8X4), rhs_scale=w_scales[:, g, lo:hi],
+                        start=(g == 0), stop=(g == PASSES - 1),
+                    )
+                nc.vector.tensor_tensor(
+                    out=result[:, lo:hi], in0=acc[:, 0 : hi - lo], in1=tok_b2[:, m, lo:hi], op=ALU.add
+                )
+            nc.sync.dma_start(out=out_rows[rows, :], in_=result[:])

@@ -112,8 +112,6 @@ def tile_shiftedpatchtokenization_pb_kernel(tc, x, ln2_g, ln2_b, w2_words, w2_sc
         nc.vector.memset(cell_sq[:], 0.0)
 
         tok_b2 = keep.tile([P, TOKEN_TILES, DIM], F32)
-        for m in range(TOKEN_TILES):
-            nc.gpsimd.tensor_tensor(out=tok_b2[:, m, :], in0=tok_bf[:, m, :], in1=b2_bf[:], op=ALU.add)
 
         hw = keep.tile([P, 16, CHANNELS, 16], F32)
         for ch in range(CHANNELS):
@@ -132,6 +130,30 @@ def tile_shiftedpatchtokenization_pb_kernel(tc, x, ln2_g, ln2_b, w2_words, w2_sc
                 op=ALU.subtract,
             )
 
+        cell_banks = []
+        for jh in range(2):
+            for px in range(2):
+                bank = psum.tile([P, 512], F32, tag="bank")
+                for jl in range(4):
+                    nc.tensor.transpose(
+                        out=bank[:, P * jl : P * jl + P],
+                        in_=hw[:, 2 * (4 * jh + jl) + px].rearrange("p ch r -> p (ch r)"),
+                        identity=ident[:],
+                    )
+                cell_banks.append(bank)
+
+        def empty_cell_banks(jh, on_scalar):
+            for px in range(2):
+                by_py = cell_banks[2 * jh + px][:].rearrange("p (jl i py b) -> p py jl i b", jl=4, i=8, py=2, b=8)
+                for py in range(2):
+                    to = cells[:, py, px, PAD + 256 * jh : PAD + 256 * jh + 256].rearrange(
+                        "p (jl i b) -> p jl i b", jl=4, i=8
+                    )
+                    if on_scalar:
+                        nc.scalar.copy(out=to, in_=by_py[:, py])
+                    else:
+                        nc.vector.tensor_copy(out=to, in_=by_py[:, py])
+
         nc.vector.tensor_reduce(
             out=cell_sum[:, 1:17], in_=hw[:].rearrange("p X ch r -> p X (ch r)"), axis=AXIS.X, op=ALU.add
         )
@@ -141,6 +163,8 @@ def tile_shiftedpatchtokenization_pb_kernel(tc, x, ln2_g, ln2_b, w2_words, w2_sc
                 out=squares[:, X, :], in_=hw[:, X].rearrange("p ch r -> p (ch r)"), func=ACT.Square,
                 accum_out=cell_sq[:, 1 + X : 2 + X],
             )
+        empty_cell_banks(0, False)
+        empty_cell_banks(1, True)
         row_sums = keep.tile([P, 2, 2, 2, TOKEN_TILES], F32)
         for stat, per_cell in enumerate((cell_sum, cell_sq)):
             straddling = work.tile([P, 9], F32)
@@ -187,25 +211,6 @@ def tile_shiftedpatchtokenization_pb_kernel(tc, x, ln2_g, ln2_b, w2_words, w2_sc
                 op0=ALU.mult,
             )
 
-        for px in range(2):
-            for jh in range(2):
-                bank = psum.tile([P, 512], F32, tag="bank")
-                for jl in range(4):
-                    nc.tensor.transpose(
-                        out=bank[:, P * jl : P * jl + P],
-                        in_=hw[:, 2 * (4 * jh + jl) + px].rearrange("p ch r -> p (ch r)"),
-                        identity=ident[:],
-                    )
-                by_py = bank[:].rearrange("p (jl i py b) -> p py jl i b", jl=4, i=8, py=2, b=8)
-                for py in range(2):
-                    to = cells[:, py, px, PAD + 256 * jh : PAD + 256 * jh + 256].rearrange(
-                        "p (jl i b) -> p jl i b", jl=4, i=8
-                    )
-                    if jh == 0:
-                        nc.scalar.copy(out=to, in_=by_py[:, py])
-                    else:
-                        nc.vector.tensor_copy(out=to, in_=by_py[:, py])
-
         y = []
         for m in range(TOKEN_TILES):
             y_m = keep.tile([P, 2, 64, 20], F32, name="y%d" % m)
@@ -245,6 +250,7 @@ def tile_shiftedpatchtokenization_pb_kernel(tc, x, ln2_g, ln2_b, w2_words, w2_sc
                         bank[:].rearrange("p (th pix e) -> p th pix e", th=2, e=8),
                         rstd[:, which, m : m + 1], shift[:, m : m + 1],
                     )
+            nc.vector.tensor_tensor(out=tok_b2[:, m, :], in0=tok_bf[:, m, :], in1=b2_bf[:], op=ALU.add)
 
         z_words = keep.tile([P, PASSES, TOKENS], U32, align_bytes=64)
         z_scales = keep.tile([P, PASSES, TOKENS], U8, align_bytes=64)

@@ -102,7 +102,7 @@ def tile_shiftedpatchtokenization_pb_kernel(tc, x, ln2_g, ln2_b, w2_words, w2_sc
         nc.vector.tensor_copy(out=gain[:], in_=gain_bf[:])
         nc.vector.tensor_copy(out=offs[:], in_=offs_bf[:])
 
-        cells = keep.tile([P, 2, 2, PLANE], F32)
+        cells = keep.tile([P, 2, 2, PLANE], F32, tag="cells_then_tok_b2")
         nc.vector.memset(cells[:, :, :, 0:PAD], 0.0)
         nc.vector.memset(cells[:, :, :, PAD + TOKENS : PLANE], 0.0)
 
@@ -111,7 +111,6 @@ def tile_shiftedpatchtokenization_pb_kernel(tc, x, ln2_g, ln2_b, w2_words, w2_sc
         nc.vector.memset(cell_sum[:], 0.0)
         nc.vector.memset(cell_sq[:], 0.0)
 
-        tok_b2 = keep.tile([P, TOKEN_TILES, DIM], F32)
 
         hw = keep.tile([P, 16, CHANNELS, 16], F32)
         for ch in range(CHANNELS):
@@ -216,42 +215,44 @@ def tile_shiftedpatchtokenization_pb_kernel(tc, x, ln2_g, ln2_b, w2_words, w2_sc
             y_m = keep.tile([P, 2, 64, 20], F32, name="y%d" % m)
             y.append(y_m)
             first = PAD + P * m
-            bank = psum.tile([P, 512], F32, tag="bank")
-            quarters = bank[:].rearrange("p (th qy yy qx r) -> p th qy yy qx r", th=2, qy=2, yy=4, qx=2, r=16)
-            for qy in range(2):
-                for qx in range(2):
-                    nc.tensor.transpose(
-                        out=quarters[:, :, qy, :, qx, :], in_=cells[:, qy, qx, first : first + P], identity=sort_ch[:]
-                    )
-            scale_and_shift(
-                nc, m, y_m[:, :, :, 0:4], bank[:].rearrange("p (th pix e) -> p th pix e", th=2, e=4),
-                rstd[:, 0, m : m + 1], shift[:, m : m + 1],
-            )
             for qy in range(2):
                 for down in range(2):
                     oy = qy - 1 + 2 * down
                     py, di = oy % 2, oy // 2
                     bank = psum.tile([P, 512], F32, tag="bank")
-                    quarters = bank[:].rearrange(
-                        "p (a qx xx right e) -> p a qx xx right e", a=8, qx=2, xx=4, right=2, e=4
-                    )
+                    quarters = bank[:].rearrange("p (a right qx r) -> p a right qx r", a=8, right=2, qx=2, r=16)
                     for qx in range(2):
                         for right in range(2):
                             ox = qx - 1 + 2 * right
                             px, dj = ox % 2, ox // 2
                             start = first + 64 * dj + 8 * di
                             nc.tensor.transpose(
-                                out=quarters[:, :, qx, :, right, :], in_=cells[:, py, px, start : start + P],
+                                out=quarters[:, :, right, qx, :], in_=cells[:, py, px, start : start + P],
                                 identity=sort_ch[:],
                             )
                     which = {-1: 1, 0: 0, 1: 2}[di]
-                    scale_and_shift(
-                        nc, m, y_m[:, :, 32 * qy : 32 * qy + 32, 4 + 8 * down : 12 + 8 * down],
-                        bank[:].rearrange("p (th pix e) -> p th pix e", th=2, e=8),
-                        rstd[:, which, m : m + 1], shift[:, m : m + 1],
+                    by_right = bank[:].rearrange(
+                        "p (th yy right q e) -> p right th yy q e", th=2, yy=4, right=2, q=8, e=4
                     )
-            nc.vector.tensor_tensor(out=tok_b2[:, m, :], in0=tok_bf[:, m, :], in1=b2_bf[:], op=ALU.add)
+                    for right in range(2):
+                        s = 1 + 2 * down + right
+                        scale_and_shift(
+                            nc, m,
+                            y_m[:, :, 32 * qy : 32 * qy + 32, 4 * s : 4 * s + 4].rearrange(
+                                "p th (yy q) e -> p th yy q e", yy=4
+                            ),
+                            by_right[:, right], rstd[:, which, m : m + 1], shift[:, m : m + 1],
+                        )
+                    if di == 0:
+                        middle = bank[:].rearrange("p (th yy c) -> p th yy c", th=2, yy=4)[:, :, :, 16:48]
+                        scale_and_shift(
+                            nc, m,
+                            y_m[:, :, 32 * oy : 32 * oy + 32, 0:4].rearrange("p th (yy q) e -> p th yy q e", yy=4),
+                            middle.rearrange("p th yy (q e) -> p th yy q e", e=4),
+                            rstd[:, 0, m : m + 1], shift[:, m : m + 1],
+                        )
 
+        tok_b2 = keep.tile([P, TOKEN_TILES, DIM], F32, tag="cells_then_tok_b2")
         z_words = keep.tile([P, PASSES, TOKENS], U32, align_bytes=64)
         z_scales = keep.tile([P, PASSES, TOKENS], U8, align_bytes=64)
         for g in range(PASSES):
@@ -284,6 +285,7 @@ def tile_shiftedpatchtokenization_pb_kernel(tc, x, ln2_g, ln2_b, w2_words, w2_sc
         for m in range(TOKEN_TILES):
             rows = slice(P * m, P * m + P)
             result = work.tile([P, DIM], F32)
+            nc.vector.tensor_tensor(out=tok_b2[:, m, :], in0=tok_bf[:, m, :], in1=b2_bf[:], op=ALU.add)
             for lo, hi in N_CUTS:
                 acc = psum.tile([P, 512], F32, tag="bank")
                 for g in range(PASSES):

@@ -102,7 +102,7 @@ def tile_shiftedpatchtokenization_pb_kernel(tc, x, ln2_g, ln2_b, w2_words, w2_sc
         nc.vector.tensor_copy(out=gain[:], in_=gain_bf[:])
         nc.vector.tensor_copy(out=offs[:], in_=offs_bf[:])
 
-        cells = keep.tile([P, 2, 2, PLANE], F32, tag="cells_then_tok_b2")
+        cells = keep.tile([P, 2, 2, PLANE], F32)
         nc.vector.memset(cells[:, :, :, 0:PAD], 0.0)
         nc.vector.memset(cells[:, :, :, PAD + TOKENS : PLANE], 0.0)
 
@@ -188,7 +188,7 @@ def tile_shiftedpatchtokenization_pb_kernel(tc, x, ln2_g, ln2_b, w2_words, w2_sc
                 rhs=row_sums[:, kind, jlo].rearrange("p s m -> p (s m)"),
                 start=(step == 0), stop=(step == 3),
             )
-        mean = keep.tile([P, TOKEN_TILES], F32)
+        mean = keep.tile([P, TOKEN_TILES], F32, tag="mean_then_tok_b2")
         spread = keep.tile([P, TOKEN_TILES], F32)
         mean_sq = keep.tile([P, TOKEN_TILES], F32)
         nc.vector.tensor_scalar(out=mean[:], in0=totals[:, 0:4], scalar1=1.0 / K, scalar2=None, op0=ALU.mult)
@@ -209,6 +209,10 @@ def tile_shiftedpatchtokenization_pb_kernel(tc, x, ln2_g, ln2_b, w2_words, w2_sc
                 out=rstd[:, 1 + edge, :], in0=rstd[:, 0, :], scalar1=inside[:, edge : edge + 1], scalar2=None,
                 op0=ALU.mult,
             )
+
+        tok_b2 = keep.tile([P, TOKEN_TILES, DIM], F32, tag="mean_then_tok_b2")
+        for m in range(TOKEN_TILES):
+            nc.gpsimd.tensor_tensor(out=tok_b2[:, m, :], in0=tok_bf[:, m, :], in1=b2_bf[:], op=ALU.add)
 
         y = []
         for m in range(TOKEN_TILES):
@@ -252,7 +256,6 @@ def tile_shiftedpatchtokenization_pb_kernel(tc, x, ln2_g, ln2_b, w2_words, w2_sc
                             rstd[:, 0, m : m + 1], shift[:, m : m + 1],
                         )
 
-        tok_b2 = keep.tile([P, TOKEN_TILES, DIM], F32, tag="cells_then_tok_b2")
         z_words = keep.tile([P, PASSES, TOKENS], U32, align_bytes=64)
         z_scales = keep.tile([P, PASSES, TOKENS], U8, align_bytes=64)
         for g in range(PASSES):
@@ -285,7 +288,6 @@ def tile_shiftedpatchtokenization_pb_kernel(tc, x, ln2_g, ln2_b, w2_words, w2_sc
         for m in range(TOKEN_TILES):
             rows = slice(P * m, P * m + P)
             result = work.tile([P, DIM], F32)
-            nc.vector.tensor_tensor(out=tok_b2[:, m, :], in0=tok_bf[:, m, :], in1=b2_bf[:], op=ALU.add)
             for lo, hi in N_CUTS:
                 acc = psum.tile([P, 512], F32, tag="bank")
                 for g in range(PASSES):

@@ -23,6 +23,7 @@ N_CUTS = ((0, 512), (512, 768))
 PAD = 72
 PLANE = PAD + TOKENS + PAD
 EPS_36 = 36.0 * 1e-5
+SQUARES_ON_SCALAR = 12
 
 FLOPS = 2 * TOKENS * K * DIM
 
@@ -70,6 +71,8 @@ def tile_shiftedpatchtokenization_pb_kernel(tc, x, ln2_g, ln2_b, w2_words, w2_sc
 
         ident = keep.tile([P, P], F32)
         make_identity(nc, ident[:])
+        neg_ident = keep.tile([P, P], BF16)
+        nc.vector.tensor_scalar(out=neg_ident[:], in0=ident[:], scalar1=-1.0, scalar2=None, op0=ALU.mult)
 
         sort_ch = keep.tile([P, P], F32)
         sort_view = sort_ch[:].rearrange("p (th r chh tl) -> p th r chh tl", th=2, r=16, chh=2, tl=2)
@@ -97,11 +100,6 @@ def tile_shiftedpatchtokenization_pb_kernel(tc, x, ln2_g, ln2_b, w2_words, w2_sc
         inside = keep.tile([P, 2], F32)
         nc.vector.tensor_scalar(out=inside[:], in0=at_edge[:], scalar1=-1.0, scalar2=1.0, op0=ALU.mult, op1=ALU.add)
 
-        gain = keep.tile([P, PASSES, PACK], F32)
-        offs = keep.tile([P, PASSES, PACK], F32)
-        nc.vector.tensor_copy(out=gain[:], in_=gain_bf[:])
-        nc.vector.tensor_copy(out=offs[:], in_=offs_bf[:])
-
         cells = keep.tile([P, 2, 2, PLANE], F32)
         nc.vector.memset(cells[:, :, :, 0:PAD], 0.0)
         nc.vector.memset(cells[:, :, :, PAD + TOKENS : PLANE], 0.0)
@@ -113,21 +111,38 @@ def tile_shiftedpatchtokenization_pb_kernel(tc, x, ln2_g, ln2_b, w2_words, w2_sc
 
 
         hw = keep.tile([P, 16, CHANNELS, 16], F32)
+        half_sums = keep.tile([P, 2, 16], F32)
+
+        def sum_half_of_the_channels(half):
+            nc.vector.tensor_reduce(
+                out=half_sums[:, half, :],
+                in_=hw[:, :, 4 * half : 4 * half + 4, :].rearrange("p X ch r -> p X (ch r)"), axis=AXIS.X, op=ALU.add,
+            )
+
         for ch in range(CHANNELS):
             blocks = x_sb[:, ch, :].rearrange("p (yy ry c rx) -> p yy ry c rx", yy=4, ry=2, c=64, rx=2)
-            upper = work.tile([P, 4, 64], F32)
-            lower = work.tile([P, 4, 64], F32)
-            nc.vector.scalar_tensor_tensor(
-                out=upper[:], in0=blocks[:, :, 0, :, 0], scalar=3.0, in1=blocks[:, :, 0, :, 1],
-                op0=ALU.mult, op1=ALU.subtract,
-            )
-            nc.vector.tensor_tensor(out=lower[:], in0=blocks[:, :, 1, :, 0], in1=blocks[:, :, 1, :, 1], op=ALU.add)
+            others = ((1, 0), (1, 1)) if ch == 0 else ((0, 1), (1, 0), (1, 1))
+            minus = psum.tile([P, 512], F32, tag="bank")
+            for n, (ry, rx) in enumerate(others):
+                nc.tensor.matmul(
+                    out=minus[:, 0:256].rearrange("p (yy c) -> p yy c", yy=4), lhsT=neg_ident[:],
+                    rhs=blocks[:, :, ry, :, rx], start=(n == 0), stop=(n == len(others) - 1),
+                )
+            hw_ch = hw[:, :, ch, :].rearrange("p X (yy xx) -> p X yy xx", yy=4)
+            minus_ch = minus[:, 0:256].rearrange("p (yy X xx) -> p X yy xx", yy=4, xx=4)
+            upper = work.tile([P, 4, 64], F32, bufs=4)
+            if ch == 0:
+                nc.vector.scalar_tensor_tensor(
+                    out=upper[:], in0=blocks[:, :, 0, :, 0], scalar=3.0, in1=blocks[:, :, 0, :, 1],
+                    op0=ALU.mult, op1=ALU.subtract,
+                )
+            else:
+                nc.scalar.activation(out=upper[:], in_=blocks[:, :, 0, :, 0], func=ACT.Copy, scale=3.0)
             nc.vector.tensor_tensor(
-                out=hw[:, :, ch, :].rearrange("p X (yy xx) -> p X yy xx", yy=4),
-                in0=upper[:].rearrange("p yy (X xx) -> p X yy xx", xx=4),
-                in1=lower[:].rearrange("p yy (X xx) -> p X yy xx", xx=4),
-                op=ALU.subtract,
+                out=hw_ch, in0=upper[:].rearrange("p yy (X xx) -> p X yy xx", xx=4), in1=minus_ch, op=ALU.add
             )
+            if ch == CHANNELS // 2 - 1:
+                sum_half_of_the_channels(0)
 
         cell_banks = []
         for jh in range(2):
@@ -153,15 +168,20 @@ def tile_shiftedpatchtokenization_pb_kernel(tc, x, ln2_g, ln2_b, w2_words, w2_sc
                     else:
                         nc.vector.tensor_copy(out=to, in_=by_py[:, py])
 
-        nc.vector.tensor_reduce(
-            out=cell_sum[:, 1:17], in_=hw[:].rearrange("p X ch r -> p X (ch r)"), axis=AXIS.X, op=ALU.add
-        )
+        sum_half_of_the_channels(1)
+        nc.vector.tensor_tensor(out=cell_sum[:, 1:17], in0=half_sums[:, 0, :], in1=half_sums[:, 1, :], op=ALU.add)
         squares = keep.tile([P, 16, P], F32)
         for X in range(16):
-            nc.scalar.activation(
-                out=squares[:, X, :], in_=hw[:, X].rearrange("p ch r -> p (ch r)"), func=ACT.Square,
-                accum_out=cell_sq[:, 1 + X : 2 + X],
-            )
+            cell = hw[:, X].rearrange("p ch r -> p (ch r)")
+            if X < SQUARES_ON_SCALAR:
+                nc.scalar.activation(
+                    out=squares[:, X, :], in_=cell, func=ACT.Square, accum_out=cell_sq[:, 1 + X : 2 + X]
+                )
+            else:
+                nc.vector.scalar_tensor_tensor(
+                    out=squares[:, X, :], in0=cell, scalar=1.0, in1=cell, op0=ALU.mult, op1=ALU.mult,
+                    accum_out=cell_sq[:, 1 + X : 2 + X],
+                )
         empty_cell_banks(0, False)
         empty_cell_banks(1, True)
         row_sums = keep.tile([P, 2, 2, 2, TOKEN_TILES], F32)
@@ -188,21 +208,21 @@ def tile_shiftedpatchtokenization_pb_kernel(tc, x, ln2_g, ln2_b, w2_words, w2_sc
                 rhs=row_sums[:, kind, jlo].rearrange("p s m -> p (s m)"),
                 start=(step == 0), stop=(step == 3),
             )
-        mean = keep.tile([P, TOKEN_TILES], F32, tag="mean_then_tok_b2")
+        means = keep.tile([P, 2, TOKEN_TILES], F32, tag="means_then_tok_b2")
+        mean = means[:, 0, :]
         spread = keep.tile([P, TOKEN_TILES], F32)
         mean_sq = keep.tile([P, TOKEN_TILES], F32)
-        nc.vector.tensor_scalar(out=mean[:], in0=totals[:, 0:4], scalar1=1.0 / K, scalar2=None, op0=ALU.mult)
         nc.vector.tensor_scalar(
-            out=spread[:], in0=totals[:, 4:8], scalar1=1.0 / K, scalar2=EPS_36, op0=ALU.mult, op1=ALU.add
+            out=means[:].rearrange("p s m -> p (s m)"), in0=totals[:, 0:8], scalar1=1.0 / K, scalar2=None, op0=ALU.mult
         )
-        nc.vector.tensor_tensor(out=mean_sq[:], in0=mean[:], in1=mean[:], op=ALU.mult)
-        nc.vector.tensor_tensor(out=spread[:], in0=spread[:], in1=mean_sq[:], op=ALU.subtract)
-        nc.scalar.activation(out=spread[:], in_=spread[:], func=ACT.Sqrt)
+        nc.vector.tensor_tensor(out=mean_sq[:], in0=mean, in1=mean, op=ALU.mult)
+        nc.vector.tensor_tensor(out=spread[:], in0=means[:, 1, :], in1=mean_sq[:], op=ALU.subtract)
+        nc.scalar.activation(out=spread[:], in_=spread[:], func=ACT.Sqrt, bias=EPS_36)
         rstd = keep.tile([P, 3, TOKEN_TILES], F32)
         shift = keep.tile([P, TOKEN_TILES], F32)
         nc.vector.reciprocal(out=rstd[:, 0, :], in_=spread[:])
         nc.vector.scalar_tensor_tensor(
-            out=shift[:], in0=mean[:], scalar=-1.0, in1=rstd[:, 0, :], op0=ALU.mult, op1=ALU.mult
+            out=shift[:], in0=mean, scalar=-1.0, in1=rstd[:, 0, :], op0=ALU.mult, op1=ALU.mult
         )
         for edge in range(2):
             nc.vector.tensor_scalar(
@@ -210,7 +230,7 @@ def tile_shiftedpatchtokenization_pb_kernel(tc, x, ln2_g, ln2_b, w2_words, w2_sc
                 op0=ALU.mult,
             )
 
-        tok_b2 = keep.tile([P, TOKEN_TILES, DIM], F32, tag="mean_then_tok_b2")
+        tok_b2 = keep.tile([P, TOKEN_TILES, DIM], F32, tag="means_then_tok_b2")
         for m in range(TOKEN_TILES):
             nc.gpsimd.tensor_tensor(out=tok_b2[:, m, :], in0=tok_bf[:, m, :], in1=b2_bf[:], op=ALU.add)
 
@@ -219,9 +239,9 @@ def tile_shiftedpatchtokenization_pb_kernel(tc, x, ln2_g, ln2_b, w2_words, w2_sc
             y_m = keep.tile([P, 2, 64, 20], F32, name="y%d" % m)
             y.append(y_m)
             first = PAD + P * m
-            for qy in range(2):
-                for down in range(2):
-                    oy = qy - 1 + 2 * down
+            for oy in (0, 1, -1, 2):
+                for down in ((oy + 1) // 2,):
+                    qy = oy + 1 - 2 * down
                     py, di = oy % 2, oy // 2
                     bank = psum.tile([P, 512], F32, tag="bank")
                     quarters = bank[:].rearrange("p (a right qx r) -> p a right qx r", a=8, right=2, qx=2, r=16)
@@ -256,6 +276,10 @@ def tile_shiftedpatchtokenization_pb_kernel(tc, x, ln2_g, ln2_b, w2_words, w2_sc
                             rstd[:, 0, m : m + 1], shift[:, m : m + 1],
                         )
 
+        gain = keep.tile([P, PASSES, PACK], F32)
+        offs = keep.tile([P, PASSES, PACK], F32)
+        nc.gpsimd.tensor_copy(out=gain[:], in_=gain_bf[:])
+        nc.gpsimd.tensor_copy(out=offs[:], in_=offs_bf[:])
         z_words = keep.tile([P, PASSES, TOKENS], U32, align_bytes=64)
         z_scales = keep.tile([P, PASSES, TOKENS], U8, align_bytes=64)
         for g in range(PASSES):

@@ -293,10 +293,10 @@ def tile_shiftedpatchtokenization_pb_kernel(tc, x, ln2_g, ln2_b, w2_words, w2_sc
                         out=bank[:, P * m : P * m + P], in_=half[:, 256 * g + tl : 256 * g + 256 : 2],
                         identity=ident[:],
                     )
-                nc.scalar.activation(
-                    out=z_planes[:, t, :].rearrange("p (b i j) -> p b i j", b=8, i=8),
-                    in_=bank[:].rearrange("p (j i b) -> p b i j", j=8, i=8),
-                    func=ACT.Identity, bias=offs[:, g, t : t + 1], scale=gain[:, g, t : t + 1],
+                scale_and_shift(
+                    nc, 1 if t == 1 else 0, z_planes[:, t, :].rearrange("p (b i j) -> p b i j", b=8, i=8),
+                    bank[:].rearrange("p (j i b) -> p b i j", j=8, i=8),
+                    gain[:, g, t : t + 1], offs[:, g, t : t + 1],
                 )
             z_grouped = work.tile([P, TOKENS, PACK], BF16, align_bytes=64)
             nc.vector.tensor_copy(

@@ -240,41 +240,45 @@ def tile_shiftedpatchtokenization_pb_kernel(tc, x, ln2_g, ln2_b, w2_words, w2_sc
             y.append(y_m)
             first = PAD + P * m
             for oy in (0, 1, -1, 2):
-                for down in ((oy + 1) // 2,):
-                    qy = oy + 1 - 2 * down
-                    py, di = oy % 2, oy // 2
-                    bank = psum.tile([P, 512], F32, tag="bank")
-                    quarters = bank[:].rearrange("p (a right qx r) -> p a right qx r", a=8, right=2, qx=2, r=16)
-                    for qx in range(2):
-                        for right in range(2):
-                            ox = qx - 1 + 2 * right
-                            px, dj = ox % 2, ox // 2
-                            start = first + 64 * dj + 8 * di
-                            nc.tensor.transpose(
-                                out=quarters[:, :, right, qx, :], in_=cells[:, py, px, start : start + P],
-                                identity=sort_ch[:],
-                            )
-                    which = {-1: 1, 0: 0, 1: 2}[di]
-                    by_right = bank[:].rearrange(
-                        "p (th yy right q e) -> p right th yy q e", th=2, yy=4, right=2, q=8, e=4
-                    )
+                down = (oy + 1) // 2
+                qy = oy + 1 - 2 * down
+                py, di = oy % 2, oy // 2
+                bank = psum.tile([P, 512], F32, tag="bank")
+                if di == 0:
+                    quarters = bank[:].rearrange("p (a right qx xx e) -> p a qx xx right e", a=8, right=2, qx=2, xx=4)
+                else:
+                    quarters = bank[:].rearrange("p (a qx xx right e) -> p a qx xx right e", a=8, qx=2, xx=4, right=2)
+                for qx in range(2):
                     for right in range(2):
-                        s = 1 + 2 * down + right
-                        scale_and_shift(
-                            nc, m,
-                            y_m[:, :, 32 * qy : 32 * qy + 32, 4 * s : 4 * s + 4].rearrange(
-                                "p th (yy q) e -> p th yy q e", yy=4
-                            ),
-                            by_right[:, right], rstd[:, which, m : m + 1], shift[:, m : m + 1],
+                        ox = qx - 1 + 2 * right
+                        px, dj = ox % 2, ox // 2
+                        start = first + 64 * dj + 8 * di
+                        nc.tensor.transpose(
+                            out=quarters[:, :, qx, :, right, :], in_=cells[:, py, px, start : start + P],
+                            identity=sort_ch[:],
                         )
-                    if di == 0:
-                        middle = bank[:].rearrange("p (th yy c) -> p th yy c", th=2, yy=4)[:, :, :, 16:48]
-                        scale_and_shift(
-                            nc, m,
-                            y_m[:, :, 32 * oy : 32 * oy + 32, 0:4].rearrange("p th (yy q) e -> p th yy q e", yy=4),
-                            middle.rearrange("p th yy (q e) -> p th yy q e", e=4),
-                            rstd[:, 0, m : m + 1], shift[:, m : m + 1],
-                        )
+                if di != 0:
+                    scale_and_shift(
+                        nc, m, y_m[:, :, 32 * qy : 32 * qy + 32, 4 + 8 * down : 12 + 8 * down],
+                        bank[:].rearrange("p (th pix e) -> p th pix e", th=2, e=8),
+                        rstd[:, {-1: 1, 1: 2}[di], m : m + 1], shift[:, m : m + 1],
+                    )
+                    continue
+                by_right = bank[:].rearrange("p (th yy right q e) -> p right th yy q e", th=2, yy=4, right=2, q=8, e=4)
+                for right in range(2):
+                    s = 1 + 2 * down + right
+                    scale_and_shift(
+                        nc, m,
+                        y_m[:, :, 32 * qy : 32 * qy + 32, 4 * s : 4 * s + 4].rearrange("p th (yy q) e -> p th yy q e", yy=4),
+                        by_right[:, right], rstd[:, 0, m : m + 1], shift[:, m : m + 1],
+                    )
+                middle = bank[:].rearrange("p (th yy c) -> p th yy c", th=2, yy=4)[:, :, :, 16:48]
+                scale_and_shift(
+                    nc, m,
+                    y_m[:, :, 32 * oy : 32 * oy + 32, 0:4].rearrange("p th (yy q) e -> p th yy q e", yy=4),
+                    middle.rearrange("p th yy (q e) -> p th yy q e", e=4),
+                    rstd[:, 0, m : m + 1], shift[:, m : m + 1],
+                )
 
         gain = keep.tile([P, PASSES, PACK], F32)
         offs = keep.tile([P, PASSES, PACK], F32)
@@ -282,31 +286,39 @@ def tile_shiftedpatchtokenization_pb_kernel(tc, x, ln2_g, ln2_b, w2_words, w2_sc
         nc.gpsimd.tensor_copy(out=offs[:], in_=offs_bf[:])
         z_words = keep.tile([P, PASSES, TOKENS], U32, align_bytes=64)
         z_scales = keep.tile([P, PASSES, TOKENS], U8, align_bytes=64)
-        for g in range(PASSES):
-            z_planes = work.tile([P, PACK, TOKENS], BF16)
-            for t in range(PACK):
-                th, tl = t // 2, t % 2
-                bank = psum.tile([P, 512], F32, tag="bank")
-                for m in range(TOKEN_TILES):
-                    half = y[m][:, th].rearrange("p pix e -> p (pix e)")
-                    nc.tensor.transpose(
-                        out=bank[:, P * m : P * m + P], in_=half[:, 256 * g + tl : 256 * g + 256 : 2],
-                        identity=ident[:],
-                    )
-                scale_and_shift(
-                    nc, 1 if t == 1 else 0, z_planes[:, t, :].rearrange("p (b i j) -> p b i j", b=8, i=8),
-                    bank[:].rearrange("p (j i b) -> p b i j", j=8, i=8),
-                    gain[:, g, t : t + 1], offs[:, g, t : t + 1],
-                )
-            z_grouped = work.tile([P, TOKENS, PACK], BF16, align_bytes=64)
-            nc.vector.tensor_copy(
-                out=z_grouped[:].rearrange("p (c i) t -> p c t i", i=4),
-                in_=z_planes[:].rearrange("p t (c i) -> p c t i", i=4),
-            )
+        def quantise(g, z_grouped):
             nc.vector.quantize_mx(
                 out=z_words[:, g, :].bitcast(FP8X4), scales=z_scales[:, g, :],
                 in_=z_grouped[:].rearrange("p n t -> p (n t)"),
             )
+
+        with tc.manual_schedule(engines={mybir.EngineType.DVE}):
+            waiting = []
+            for g in range(PASSES):
+                z_planes = work.tile([P, PACK, TOKENS], BF16)
+                for t in range(PACK):
+                    th, tl = t // 2, t % 2
+                    bank = psum.tile([P, 512], F32, tag="bank")
+                    for m in range(TOKEN_TILES):
+                        half = y[m][:, th].rearrange("p pix e -> p (pix e)")
+                        nc.tensor.transpose(
+                            out=bank[:, P * m : P * m + P], in_=half[:, 256 * g + tl : 256 * g + 256 : 2],
+                            identity=ident[:],
+                        )
+                    scale_and_shift(
+                        nc, 1 if t == 1 else 0, z_planes[:, t, :].rearrange("p (b i j) -> p b i j", b=8, i=8),
+                        bank[:].rearrange("p (j i b) -> p b i j", j=8, i=8),
+                        gain[:, g, t : t + 1], offs[:, g, t : t + 1],
+                    )
+                    if t == 1 and waiting:
+                        quantise(g - 1, waiting.pop())
+                z_grouped = work.tile([P, TOKENS, PACK], BF16, align_bytes=64)
+                nc.vector.tensor_copy(
+                    out=z_grouped[:].rearrange("p (c i) t -> p c t i", i=4),
+                    in_=z_planes[:].rearrange("p t (c i) -> p c t i", i=4),
+                )
+                waiting.append(z_grouped)
+            quantise(PASSES - 1, waiting.pop())
 
         out_rows = out.flatten_outer_dims()
         for m in range(TOKEN_TILES):

@@ -306,7 +306,7 @@ def tile_shiftedpatchtokenization_pb_kernel(tc, x, ln2_g, ln2_b, w2_words, w2_sc
                             identity=ident[:],
                         )
                     scale_and_shift(
-                        nc, 1 if t == 1 else 0, z_planes[:, t, :].rearrange("p (b i j) -> p b i j", b=8, i=8),
+                        nc, 1 if (t == 1 and g % 2 == 0) else 0, z_planes[:, t, :].rearrange("p (b i j) -> p b i j", b=8, i=8),
                         bank[:].rearrange("p (j i b) -> p b i j", j=8, i=8),
                         gain[:, g, t : t + 1], offs[:, g, t : t + 1],
                     )

@@ -44,6 +44,11 @@ def tile_shiftedpatchtokenization_pb_kernel(tc, x, ln2_g, ln2_b, w2_words, w2_sc
         for ch in range(CHANNELS):
             nc.sync.dma_start(out=x_sb[:, ch, :], in_=x[:, ch].rearrange("b (iy r) w -> iy b (r w)", r=8))
 
+        tok_bf = keep.tile([P, TOKEN_TILES, DIM], BF16)
+        nc.sync.dma_start(out=tok_bf[:], in_=tok.flatten_outer_dims().rearrange("(m p) n -> p m n", p=P))
+        b2_bf = keep.tile([P, DIM], BF16)
+        nc.sync.dma_start(out=b2_bf[:], in_=b2.partition_broadcast(P))
+
         gain_bf = keep.tile([P, PASSES, PACK], BF16)
         offs_bf = keep.tile([P, PASSES, PACK], BF16)
         nc.sync.dma_start(out=gain_bf[:], in_=ln2_g.rearrange("(g p t) -> p g t", g=PASSES, p=P))
@@ -60,10 +65,6 @@ def tile_shiftedpatchtokenization_pb_kernel(tc, x, ln2_g, ln2_b, w2_words, w2_sc
         nc.sync.dma_start(
             out=w_words[:].bitcast(I32), in_=w2_words.rearrange("g p n t -> p g (n t)").bitcast(I32)
         )
-        tok_bf = keep.tile([P, TOKEN_TILES, DIM], BF16)
-        nc.sync.dma_start(out=tok_bf[:], in_=tok.flatten_outer_dims().rearrange("(m p) n -> p m n", p=P))
-        b2_bf = keep.tile([P, DIM], BF16)
-        nc.sync.dma_start(out=b2_bf[:], in_=b2.partition_broadcast(P))
 
         one = keep.tile([P, 1], F32)
         nc.vector.memset(one[:], 1.0)
@@ -158,15 +159,12 @@ def tile_shiftedpatchtokenization_pb_kernel(tc, x, ln2_g, ln2_b, w2_words, w2_sc
 
         def empty_cell_banks(jh, on_scalar):
             for px in range(2):
-                by_py = cell_banks[2 * jh + px][:].rearrange("p (jl i py b) -> p py jl i b", jl=4, i=8, py=2, b=8)
-                for py in range(2):
-                    to = cells[:, py, px, PAD + 256 * jh : PAD + 256 * jh + 256].rearrange(
-                        "p (jl i b) -> p jl i b", jl=4, i=8
-                    )
-                    if on_scalar:
-                        nc.scalar.copy(out=to, in_=by_py[:, py])
-                    else:
-                        nc.vector.tensor_copy(out=to, in_=by_py[:, py])
+                by_py = cell_banks[2 * jh + px][:].rearrange("p (ji py b) -> p py ji b", ji=32, py=2, b=8)
+                to = cells[:, :, px, PAD + 256 * jh : PAD + 256 * jh + 256].rearrange("p py (ji b) -> p py ji b", b=8)
+                if on_scalar:
+                    nc.scalar.copy(out=to, in_=by_py)
+                else:
+                    nc.vector.tensor_copy(out=to, in_=by_py)
 
         sum_half_of_the_channels(1)
         nc.vector.tensor_tensor(out=cell_sum[:, 1:17], in0=half_sums[:, 0, :], in1=half_sums[:, 1, :], op=ALU.add)
@@ -336,4 +334,4 @@ def tile_shiftedpatchtokenization_pb_kernel(tc, x, ln2_g, ln2_b, w2_words, w2_sc
                 nc.vector.tensor_tensor(
                     out=result[:, lo:hi], in0=acc[:, 0 : hi - lo], in1=tok_b2[:, m, lo:hi], op=ALU.add
                 )
-            nc.sync.dma_start(out=out_rows[rows, :], in_=result[:])
+                nc.sync.dma_start(out=out_rows[rows, lo:hi], in_=result[:, lo:hi])

@@ -23,6 +23,7 @@ N_CUTS = ((0, 512), (512, 768))
 PAD = 72
 PLANE = PAD + TOKENS + PAD
 EPS_36 = 36.0 * 1e-5
+FIRST_TILES = 2
 SQUARES_ON_SCALAR = 12
 
 FLOPS = 2 * TOKENS * K * DIM
@@ -157,14 +158,13 @@ def tile_shiftedpatchtokenization_pb_kernel(tc, x, ln2_g, ln2_b, w2_words, w2_sc
                     )
                 cell_banks.append(bank)
 
-        def empty_cell_banks(jh, on_scalar):
-            for px in range(2):
-                by_py = cell_banks[2 * jh + px][:].rearrange("p (ji py b) -> p py ji b", ji=32, py=2, b=8)
-                to = cells[:, :, px, PAD + 256 * jh : PAD + 256 * jh + 256].rearrange("p py (ji b) -> p py ji b", b=8)
-                if on_scalar:
-                    nc.scalar.copy(out=to, in_=by_py)
-                else:
-                    nc.vector.tensor_copy(out=to, in_=by_py)
+        def empty_cell_bank(jh, px, on_scalar):
+            by_py = cell_banks[2 * jh + px][:].rearrange("p (ji py b) -> p py ji b", ji=32, py=2, b=8)
+            to = cells[:, :, px, PAD + 256 * jh : PAD + 256 * jh + 256].rearrange("p py (ji b) -> p py ji b", b=8)
+            if on_scalar:
+                nc.scalar.copy(out=to, in_=by_py)
+            else:
+                nc.vector.tensor_copy(out=to, in_=by_py)
 
         sum_half_of_the_channels(1)
         nc.vector.tensor_tensor(out=cell_sum[:, 1:17], in0=half_sums[:, 0, :], in1=half_sums[:, 1, :], op=ALU.add)
@@ -180,8 +180,8 @@ def tile_shiftedpatchtokenization_pb_kernel(tc, x, ln2_g, ln2_b, w2_words, w2_sc
                     out=squares[:, X, :], in0=cell, scalar=1.0, in1=cell, op0=ALU.mult, op1=ALU.mult,
                     accum_out=cell_sq[:, 1 + X : 2 + X],
                 )
-        empty_cell_banks(0, False)
-        empty_cell_banks(1, True)
+        empty_cell_bank(0, 0, True)
+        empty_cell_bank(0, 1, True)
         row_sums = keep.tile([P, 2, 2, 2, TOKEN_TILES], F32)
         for stat, per_cell in enumerate((cell_sum, cell_sq)):
             straddling = work.tile([P, 9], F32)
@@ -206,6 +206,7 @@ def tile_shiftedpatchtokenization_pb_kernel(tc, x, ln2_g, ln2_b, w2_words, w2_sc
                 rhs=row_sums[:, kind, jlo].rearrange("p s m -> p (s m)"),
                 start=(step == 0), stop=(step == 3),
             )
+        empty_cell_bank(1, 0, False)
         means = keep.tile([P, 2, TOKEN_TILES], F32, tag="means_then_tok_b2")
         mean = means[:, 0, :]
         spread = keep.tile([P, TOKEN_TILES], F32)
@@ -216,6 +217,7 @@ def tile_shiftedpatchtokenization_pb_kernel(tc, x, ln2_g, ln2_b, w2_words, w2_sc
         nc.vector.tensor_tensor(out=mean_sq[:], in0=mean, in1=mean, op=ALU.mult)
         nc.vector.tensor_tensor(out=spread[:], in0=means[:, 1, :], in1=mean_sq[:], op=ALU.subtract)
         nc.scalar.activation(out=spread[:], in_=spread[:], func=ACT.Sqrt, bias=EPS_36)
+        empty_cell_bank(1, 1, True)
         rstd = keep.tile([P, 3, TOKEN_TILES], F32)
         shift = keep.tile([P, TOKEN_TILES], F32)
         nc.vector.reciprocal(out=rstd[:, 0, :], in_=spread[:])
@@ -319,19 +321,37 @@ def tile_shiftedpatchtokenization_pb_kernel(tc, x, ln2_g, ln2_b, w2_words, w2_sc
             quantise(PASSES - 1, waiting.pop())
 
         out_rows = out.flatten_outer_dims()
-        for m in range(TOKEN_TILES):
+
+        def mx_passes(acc, m, cut, passes):
+            lo, hi = cut
             rows = slice(P * m, P * m + P)
-            result = work.tile([P, DIM], F32)
-            for lo, hi in N_CUTS:
-                acc = psum.tile([P, 512], F32, tag="bank")
-                for g in range(PASSES):
-                    nc.tensor.matmul_mx(
-                        out=acc[:, 0 : hi - lo],
-                        lhsT=z_words[:, g, rows].bitcast(FP8X4), lhsT_scale=z_scales[:, g, rows],
-                        rhs=w_words[:, g, lo:hi].bitcast(FP8X4), rhs_scale=w_scales[:, g, lo:hi],
-                        start=(g == 0), stop=(g == PASSES - 1),
-                    )
-                nc.vector.tensor_tensor(
-                    out=result[:, lo:hi], in0=acc[:, 0 : hi - lo], in1=tok_b2[:, m, lo:hi], op=ALU.add
+            for g in passes:
+                nc.tensor.matmul_mx(
+                    out=acc[:, 0 : hi - lo],
+                    lhsT=z_words[:, g, rows].bitcast(FP8X4), lhsT_scale=z_scales[:, g, rows],
+                    rhs=w_words[:, g, lo:hi].bitcast(FP8X4), rhs_scale=w_scales[:, g, lo:hi],
+                    start=(g == 0), stop=(g == PASSES - 1),
                 )
-                nc.sync.dma_start(out=out_rows[rows, lo:hi], in_=result[:, lo:hi])
+
+        def finish(acc, m, cut):
+            lo, hi = cut
+            result = work.tile([P, 512], F32, bufs=4)
+            nc.vector.tensor_tensor(
+                out=result[:, 0 : hi - lo], in0=acc[:, 0 : hi - lo], in1=tok_b2[:, m, lo:hi], op=ALU.add
+            )
+            nc.sync.dma_start(out=out_rows[P * m : P * m + P, lo:hi], in_=result[:, 0 : hi - lo])
+
+        first_groups = []
+        for m in range(FIRST_TILES):
+            for cut in N_CUTS:
+                acc = psum.tile([P, 512], F32, tag="bank")
+                mx_passes(acc, m, cut, range(PASSES - 1))
+                first_groups.append((acc, m, cut))
+        for acc, m, cut in first_groups:
+            mx_passes(acc, m, cut, (PASSES - 1,))
+            finish(acc, m, cut)
+        for m in range(FIRST_TILES, TOKEN_TILES):
+            for cut in N_CUTS:
+                acc = psum.tile([P, 512], F32, tag="bank")
+                mx_passes(acc, m, cut, range(PASSES))
+                finish(acc, m, cut)

@@ -24,7 +24,9 @@ PAD = 72
 PLANE = PAD + TOKENS + PAD
 EPS_36 = 36.0 * 1e-5
 FIRST_TILES = 2
-SQUARES_ON_SCALAR = 12
+SQUARES_ON_SCALAR = (16, 10)
+VECTOR_COLS = 16
+HALF = P // 2
 
 FLOPS = 2 * TOKENS * K * DIM
 
@@ -41,9 +43,11 @@ def tile_shiftedpatchtokenization_pb_kernel(tc, x, ln2_g, ln2_b, w2_words, w2_sc
     with tc.tile_pool(name="keep", bufs=1) as keep, tc.tile_pool(name="work", bufs=2) as work, tc.psum_pool(
         name="psum", bufs=8
     ) as psum:
-        x_sb = keep.tile([P, CHANNELS, 1024], BF16)
-        for ch in range(CHANNELS):
-            nc.sync.dma_start(out=x_sb[:, ch, :], in_=x[:, ch].rearrange("b (iy r) w -> iy b (r w)", r=8))
+        x_sb = keep.tile([P, 2, 4, 1024], BF16)
+        for th in range(2):
+            for e in range(4):
+                channel = 4 * (e // 2) + 2 * th + e % 2
+                nc.sync.dma_start(out=x_sb[:, th, e, :], in_=x[:, channel].rearrange("b (iy r) w -> iy b (r w)", r=8))
 
         tok_bf = keep.tile([P, TOKEN_TILES, DIM], BF16)
         nc.sync.dma_start(out=tok_bf[:], in_=tok.flatten_outer_dims().rearrange("(m p) n -> p m n", p=P))
@@ -67,168 +71,157 @@ def tile_shiftedpatchtokenization_pb_kernel(tc, x, ln2_g, ln2_b, w2_words, w2_sc
             out=w_words[:].bitcast(I32), in_=w2_words.rearrange("g p n t -> p g (n t)").bitcast(I32)
         )
 
+        OUTER, OWN = 0, 1
+        pick_rows = keep.tile([P, 2, 2, 8, 8], F32)
         one = keep.tile([P, 1], F32)
-        nc.vector.memset(one[:], 1.0)
-        nc.scalar.activation(out=one[:], in_=one[:], func=ACT.Sqrt)
-
         ident = keep.tile([P, P], F32)
-        make_identity(nc, ident[:])
+        ident_k = keep.tile([P, P], F32)
         neg_ident = keep.tile([P, P], BF16)
-        nc.vector.tensor_scalar(out=neg_ident[:], in0=ident[:], scalar1=-1.0, scalar2=None, op0=ALU.mult)
-
-        sort_ch = keep.tile([P, P], F32)
-        sort_view = sort_ch[:].rearrange("p (th r chh tl) -> p th r chh tl", th=2, r=16, chh=2, tl=2)
-        ident_view = ident[:].rearrange("p (chh th tl r) -> p th r chh tl", chh=2, th=2, tl=2, r=16)
-        for th in range(2):
-            nc.vector.tensor_copy(out=sort_view[:, th], in_=ident_view[:, th])
-
-        WIDE, NEAR = 0, 1
-        pick_rows = keep.tile([P, 2, 2, 2, 8, 8], F32)
-        nc.vector.memset(pick_rows[:], 0.0)
-        by_row = ident[:].rearrange("p (i py b) -> p i py b", i=8, py=2, b=8)
-        near = pick_rows[:, NEAR, 0, 0]
-        wide = pick_rows[:, WIDE, 0, 0]
-        nc.vector.tensor_tensor(out=near, in0=by_row[:, :, 0, :], in1=by_row[:, :, 1, :], op=ALU.add)
-        nc.vector.tensor_copy(out=wide, in_=near)
-        nc.vector.tensor_tensor(out=wide[:, 1:8], in0=wide[:, 1:8], in1=by_row[:, 0:7, 1, :], op=ALU.add)
-        nc.vector.tensor_tensor(out=wide[:, 0:7], in0=wide[:, 0:7], in1=by_row[:, 1:8, 0, :], op=ALU.add)
-        nc.vector.tensor_copy(out=pick_rows[:, NEAR, 1, 1], in_=near)
-        nc.vector.tensor_copy(out=pick_rows[:, WIDE, 1, 1], in_=wide)
-
-        by_token = ident[:].rearrange("p (jlo i b) -> p jlo i b", jlo=2, i=8, b=8)
-        at_edge = keep.tile([P, 2], F32)
-        nc.vector.tensor_reduce(out=at_edge[:, 0:1], in_=by_token[:, :, 0, :], axis=AXIS.XY, op=ALU.add)
-        nc.vector.tensor_reduce(out=at_edge[:, 1:2], in_=by_token[:, :, 7, :], axis=AXIS.XY, op=ALU.add)
-        inside = keep.tile([P, 2], F32)
-        nc.vector.tensor_scalar(out=inside[:], in0=at_edge[:], scalar1=-1.0, scalar2=1.0, op0=ALU.mult, op1=ALU.add)
-
+        hw = keep.tile([P, 18, 2, 4, 16], F32)
+        parts = keep.tile([P, 2, 2, 18], F32)
         cells = keep.tile([P, 2, 2, PLANE], F32)
-        nc.vector.memset(cells[:, :, :, 0:PAD], 0.0)
-        nc.vector.memset(cells[:, :, :, PAD + TOKENS : PLANE], 0.0)
+        at_edge = keep.tile([P, 2], F32)
+        inside = keep.tile([P, 2], F32)
+        squares = keep.tile([P, 2, 16, 64], F32)
+        by_e = []
+        for th in range(2):
+            by_e.append(x_sb[:, th].rearrange("p e (h y ry c rx) -> p h y ry c rx e", h=2, y=2, ry=2, c=64, rx=2))
 
-        cell_sum = keep.tile([P, 18], F32)
-        cell_sq = keep.tile([P, 18], F32)
-        nc.vector.memset(cell_sum[:], 0.0)
-        nc.vector.memset(cell_sq[:], 0.0)
+        with tc.manual_schedule(engines={mybir.EngineType.DVE, mybir.EngineType.Pool}):
+            nc.vector.memset(one[:], 1.0)
+            nc.scalar.activation(out=one[:], in_=one[:], func=ACT.Abs_reciprocal_sqrt)
+            make_identity(nc, ident[:])
+            nc.vector.memset(parts[:], 0.0)
+            nc.vector.memset(hw[:, 0], 0.0)
+            nc.vector.memset(hw[:, 17], 0.0)
+            nc.vector.tensor_scalar(out=neg_ident[:], in0=ident[:], scalar1=-1.0, scalar2=None, op0=ALU.mult)
+            nc.vector.tensor_scalar(out=ident_k[:], in0=ident[:], scalar1=1.0 / K, scalar2=None, op0=ALU.mult)
+            by_row = ident_k[:].rearrange("p (i q b) -> p q i b", i=8, q=2, b=8)
+            outer = pick_rows[:, OUTER, 0]
+            own = pick_rows[:, OWN, 0]
+            nc.vector.tensor_tensor(out=own, in0=by_row[:, 0], in1=by_row[:, 1], op=ALU.add)
+            nc.vector.tensor_copy(out=outer, in_=own)
+            nc.vector.tensor_tensor(out=outer[:, 1:8], in0=outer[:, 1:8], in1=by_row[:, 1, 0:7], op=ALU.add)
+            nc.vector.tensor_tensor(out=outer[:, 0:7], in0=outer[:, 0:7], in1=by_row[:, 0, 1:8], op=ALU.add)
+            nc.vector.tensor_tensor(out=own, in0=own, in1=outer, op=ALU.add)
+            nc.vector.tensor_copy(out=pick_rows[:, OUTER, 1], in_=outer)
+            nc.vector.tensor_copy(out=pick_rows[:, OWN, 1], in_=own)
 
+            nc.vector.memset(cells[:, :, :, 0:PAD], 0.0)
+            nc.vector.memset(cells[:, :, :, PAD + TOKENS : PLANE], 0.0)
+            by_token = ident[:].rearrange("p (jlo i b) -> p jlo i b", jlo=2, i=8, b=8)
+            nc.vector.tensor_reduce(out=at_edge[:, 0:1], in_=by_token[:, :, 0, :], axis=AXIS.XY, op=ALU.add)
+            nc.vector.tensor_reduce(out=at_edge[:, 1:2], in_=by_token[:, :, 7, :], axis=AXIS.XY, op=ALU.add)
+            nc.vector.tensor_scalar(out=inside[:], in0=at_edge[:], scalar1=-1.0, scalar2=1.0, op0=ALU.mult, op1=ALU.add)
 
-        hw = keep.tile([P, 16, CHANNELS, 16], F32)
-        half_sums = keep.tile([P, 2, 16], F32)
-
-        def sum_half_of_the_channels(half):
-            nc.vector.tensor_reduce(
-                out=half_sums[:, half, :],
-                in_=hw[:, :, 4 * half : 4 * half + 4, :].rearrange("p X ch r -> p X (ch r)"), axis=AXIS.X, op=ALU.add,
-            )
-
-        for ch in range(CHANNELS):
-            blocks = x_sb[:, ch, :].rearrange("p (yy ry c rx) -> p yy ry c rx", yy=4, ry=2, c=64, rx=2)
-            others = ((1, 0), (1, 1)) if ch == 0 else ((0, 1), (1, 0), (1, 1))
-            minus = psum.tile([P, 512], F32, tag="bank")
-            for n, (ry, rx) in enumerate(others):
-                nc.tensor.matmul(
-                    out=minus[:, 0:256].rearrange("p (yy c) -> p yy c", yy=4), lhsT=neg_ident[:],
-                    rhs=blocks[:, :, ry, :, rx], start=(n == 0), stop=(n == len(others) - 1),
-                )
-            hw_ch = hw[:, :, ch, :].rearrange("p X (yy xx) -> p X yy xx", yy=4)
-            minus_ch = minus[:, 0:256].rearrange("p (yy X xx) -> p X yy xx", yy=4, xx=4)
-            upper = work.tile([P, 4, 64], F32, bufs=4)
-            if ch == 0:
-                nc.vector.scalar_tensor_tensor(
-                    out=upper[:], in0=blocks[:, :, 0, :, 0], scalar=3.0, in1=blocks[:, :, 0, :, 1],
-                    op0=ALU.mult, op1=ALU.subtract,
-                )
-            else:
-                nc.scalar.activation(out=upper[:], in_=blocks[:, :, 0, :, 0], func=ACT.Copy, scale=3.0)
-            nc.vector.tensor_tensor(
-                out=hw_ch, in0=upper[:].rearrange("p yy (X xx) -> p X yy xx", xx=4), in1=minus_ch, op=ALU.add
-            )
-            if ch == CHANNELS // 2 - 1:
-                sum_half_of_the_channels(0)
-
-        cell_banks = []
-        for jh in range(2):
-            for px in range(2):
-                bank = psum.tile([P, 512], F32, tag="bank")
-                for jl in range(4):
-                    nc.tensor.transpose(
-                        out=bank[:, P * jl : P * jl + P],
-                        in_=hw[:, 2 * (4 * jh + jl) + px].rearrange("p ch r -> p (ch r)"),
-                        identity=ident[:],
+            banks = []
+            uppers = []
+            for th in range(2):
+                for yyh in range(2):
+                    minus = psum.tile([P, 512], F32, tag="bank")
+                    banks.append(minus)
+                for e in range(4):
+                    blocks = x_sb[:, th, e].rearrange("p (h y ry c rx) -> p h y ry c rx", h=2, y=2, ry=2, c=64, rx=2)
+                    for yyh in range(2):
+                        unit = 2 * th + yyh
+                        cols = banks[unit][:, P * e : P * e + P].rearrange("p (y c) -> p y c", y=2)
+                        for n, (ry, rx) in enumerate(((1, 0), (0, 1), (1, 1))):
+                            skip = VECTOR_COLS if (unit, ry, rx) == (0, 0, 1) else 0
+                            nc.tensor.matmul(
+                                out=cols[:, :, skip:], lhsT=neg_ident[:], rhs=blocks[:, yyh, :, ry, skip:, rx],
+                                start=(n == 0), stop=(n == 2),
+                            )
+                for yyh in range(2):
+                    upper = work.tile([P, 2, 64, 4], F32, bufs=4)
+                    uppers.append(upper)
+                    nc.scalar.activation(out=upper[:], in_=by_e[th][:, yyh, :, 0, :, 0, :], func=ACT.Copy, scale=3.0)
+            few = uppers[0][:, :, 0:VECTOR_COLS, :]
+            nc.vector.tensor_tensor(out=few, in0=few, in1=by_e[0][:, 0, :, 0, 0:VECTOR_COLS, 1, :], op=ALU.subtract)
+            for th in range(2):
+                for yyh in range(2):
+                    unit = 2 * th + yyh
+                    hw_unit = hw[:, 1:17, th, 2 * yyh : 2 * yyh + 2, :]
+                    nc.vector.tensor_tensor(
+                        out=hw_unit.rearrange("p X y (xx e) -> p y X xx e", xx=4),
+                        in0=uppers[unit][:].rearrange("p y (X xx) e -> p y X xx e", xx=4),
+                        in1=banks[unit][:].rearrange("p (e y X xx) -> p y X xx e", e=4, y=2, xx=4),
+                        op=ALU.add,
                     )
-                cell_banks.append(bank)
+                cell_values = hw[:, 1:17, th].rearrange("p X yy r -> p X (yy r)")
+                nc.vector.tensor_reduce(out=parts[:, 0, th, 1:17], in_=cell_values, axis=AXIS.X, op=ALU.add)
+                for X in range(16):
+                    square_sum = parts[:, 1, th, 1 + X : 2 + X]
+                    if X < SQUARES_ON_SCALAR[th]:
+                        nc.scalar.activation(
+                            out=squares[:, th, X, :], in_=cell_values[:, X, :], func=ACT.Square, accum_out=square_sum
+                        )
+                    else:
+                        nc.vector.scalar_tensor_tensor(
+                            out=squares[:, th, X, :], in0=cell_values[:, X, :], scalar=1.0, in1=cell_values[:, X, :],
+                            op0=ALU.mult, op1=ALU.mult, accum_out=square_sum,
+                        )
 
-        def empty_cell_bank(jh, px, on_scalar):
-            by_py = cell_banks[2 * jh + px][:].rearrange("p (ji py b) -> p py ji b", ji=32, py=2, b=8)
-            to = cells[:, :, px, PAD + 256 * jh : PAD + 256 * jh + 256].rearrange("p py (ji b) -> p py ji b", b=8)
-            if on_scalar:
-                nc.scalar.copy(out=to, in_=by_py)
-            else:
-                nc.vector.tensor_copy(out=to, in_=by_py)
+            cell_banks = []
+            for jh in range(2):
+                for px in range(2):
+                    bank = psum.tile([P, 512], F32, tag="bank")
+                    for jl in range(4):
+                        nc.tensor.transpose(
+                            out=bank[:, P * jl : P * jl + P],
+                            in_=hw[:, 1 + 2 * (4 * jh + jl) + px].rearrange("p th yy r -> p (th yy r)"),
+                            identity=ident[:],
+                        )
+                    cell_banks.append(bank)
 
-        sum_half_of_the_channels(1)
-        nc.vector.tensor_tensor(out=cell_sum[:, 1:17], in0=half_sums[:, 0, :], in1=half_sums[:, 1, :], op=ALU.add)
-        squares = keep.tile([P, 16, P], F32)
-        for X in range(16):
-            cell = hw[:, X].rearrange("p ch r -> p (ch r)")
-            if X < SQUARES_ON_SCALAR:
-                nc.scalar.activation(
-                    out=squares[:, X, :], in_=cell, func=ACT.Square, accum_out=cell_sq[:, 1 + X : 2 + X]
-                )
-            else:
-                nc.vector.scalar_tensor_tensor(
-                    out=squares[:, X, :], in0=cell, scalar=1.0, in1=cell, op0=ALU.mult, op1=ALU.mult,
-                    accum_out=cell_sq[:, 1 + X : 2 + X],
-                )
-        empty_cell_bank(0, 0, True)
-        empty_cell_bank(0, 1, True)
-        row_sums = keep.tile([P, 2, 2, 2, TOKEN_TILES], F32)
-        for stat, per_cell in enumerate((cell_sum, cell_sq)):
-            straddling = work.tile([P, 9], F32)
-            pairs = per_cell[:].rearrange("p (J two) -> p J two", two=2)
-            nc.vector.tensor_tensor(out=straddling[:], in0=pairs[:, :, 0], in1=pairs[:, :, 1], op=ALU.add)
+            def empty_cell_bank(jh, px, on_scalar):
+                by_py = cell_banks[2 * jh + px][:].rearrange("p (ji py b) -> p py ji b", ji=32, py=2, b=8)
+                to = cells[:, :, px, PAD + 256 * jh : PAD + 256 * jh + 256].rearrange("p py (ji b) -> p py ji b", b=8)
+                if on_scalar:
+                    nc.scalar.copy(out=to, in_=by_py)
+                else:
+                    nc.vector.tensor_copy(out=to, in_=by_py)
+
+            empty_cell_bank(0, 0, True)
+            empty_cell_bank(0, 1, True)
+            row_sums = keep.tile([P, 2, 2, 2, 8], F32)
+            ends = parts[:].rearrange("p s th (J two) -> p s th J two", two=2)
             nc.vector.tensor_tensor(
-                out=row_sums[:, WIDE, :, stat, :].rearrange("p jlo m -> p m jlo"),
-                in0=straddling[:, 0:8].rearrange("p (m jlo) -> p m jlo", jlo=2),
-                in1=straddling[:, 1:9].rearrange("p (m jlo) -> p m jlo", jlo=2),
-                op=ALU.add,
+                out=row_sums[:, OUTER], in0=ends[:, :, :, 0:8, 0], in1=ends[:, :, :, 1:9, 1], op=ALU.add
             )
-            own = per_cell[:, 1:17].rearrange("p (m jlo two) -> p m jlo two", jlo=2, two=2)
             nc.vector.tensor_tensor(
-                out=row_sums[:, NEAR, :, stat, :].rearrange("p jlo m -> p m jlo"),
-                in0=own[:, :, :, 0], in1=own[:, :, :, 1], op=ALU.add,
+                out=row_sums[:, OWN], in0=ends[:, :, :, 0:8, 1], in1=ends[:, :, :, 1:9, 0], op=ALU.add
             )
-        totals = psum.tile([P, 512], F32, tag="bank")
-        for step, (kind, jlo) in enumerate(((WIDE, 0), (WIDE, 1), (NEAR, 0), (NEAR, 1))):
-            nc.tensor.matmul(
-                out=totals[:, 0:8],
-                lhsT=pick_rows[:, kind, jlo].rearrange("p a i b -> p (a i b)"),
-                rhs=row_sums[:, kind, jlo].rearrange("p s m -> p (s m)"),
-                start=(step == 0), stop=(step == 3),
+            totals = psum.tile([P, 512], F32, tag="bank")
+            for kind in (OUTER, OWN):
+                nc.tensor.matmul(
+                    out=totals[:, 0:32],
+                    lhsT=pick_rows[:, kind].rearrange("p jlo i b -> p (jlo i b)"),
+                    rhs=row_sums[:, kind].rearrange("p s th j -> p (s th j)"),
+                    start=(kind == OUTER), stop=(kind == OWN),
+                )
+            empty_cell_bank(1, 0, False)
+            means = keep.tile([P, 2, TOKEN_TILES], F32, tag="means_then_tok_b2")
+            mean = means[:, 0, :]
+            spread = keep.tile([P, TOKEN_TILES], F32)
+            mean_sq = keep.tile([P, TOKEN_TILES], F32)
+            by_jlo = totals[:, 0:32].rearrange("p (s th m jlo) -> p jlo s m th", s=2, th=2, jlo=2)
+            for jlo in range(2):
+                rows = slice(HALF * jlo, HALF * jlo + HALF)
+                nc.vector.tensor_reduce(out=means[rows], in_=by_jlo[rows, jlo], axis=AXIS.X, op=ALU.add)
+            nc.vector.tensor_tensor(out=mean_sq[:], in0=mean, in1=mean, op=ALU.mult)
+            nc.vector.tensor_tensor(out=spread[:], in0=means[:, 1, :], in1=mean_sq[:], op=ALU.subtract)
+            rstd = keep.tile([P, 3, TOKEN_TILES], F32)
+            shift = keep.tile([P, TOKEN_TILES], F32)
+            nc.scalar.activation(out=rstd[:, 0, :], in_=spread[:], func=ACT.Abs_reciprocal_sqrt, bias=EPS_36)
+            empty_cell_bank(1, 1, True)
+            nc.vector.scalar_tensor_tensor(
+                out=shift[:], in0=mean, scalar=-1.0, in1=rstd[:, 0, :], op0=ALU.mult, op1=ALU.mult
             )
-        empty_cell_bank(1, 0, False)
-        means = keep.tile([P, 2, TOKEN_TILES], F32, tag="means_then_tok_b2")
-        mean = means[:, 0, :]
-        spread = keep.tile([P, TOKEN_TILES], F32)
-        mean_sq = keep.tile([P, TOKEN_TILES], F32)
-        nc.vector.tensor_scalar(
-            out=means[:].rearrange("p s m -> p (s m)"), in0=totals[:, 0:8], scalar1=1.0 / K, scalar2=None, op0=ALU.mult
-        )
-        nc.vector.tensor_tensor(out=mean_sq[:], in0=mean, in1=mean, op=ALU.mult)
-        nc.vector.tensor_tensor(out=spread[:], in0=means[:, 1, :], in1=mean_sq[:], op=ALU.subtract)
-        nc.scalar.activation(out=spread[:], in_=spread[:], func=ACT.Sqrt, bias=EPS_36)
-        empty_cell_bank(1, 1, True)
-        rstd = keep.tile([P, 3, TOKEN_TILES], F32)
-        shift = keep.tile([P, TOKEN_TILES], F32)
-        nc.vector.reciprocal(out=rstd[:, 0, :], in_=spread[:])
-        nc.vector.scalar_tensor_tensor(
-            out=shift[:], in0=mean, scalar=-1.0, in1=rstd[:, 0, :], op0=ALU.mult, op1=ALU.mult
-        )
-        for edge in range(2):
-            nc.vector.tensor_scalar(
-                out=rstd[:, 1 + edge, :], in0=rstd[:, 0, :], scalar1=inside[:, edge : edge + 1], scalar2=None,
-                op0=ALU.mult,
-            )
+            for edge in range(2):
+                nc.vector.tensor_scalar(
+                    out=rstd[:, 1 + edge, :], in0=rstd[:, 0, :], scalar1=inside[:, edge : edge + 1], scalar2=None,
+                    op0=ALU.mult,
+                )
 
         tok_b2 = keep.tile([P, TOKEN_TILES, DIM], F32, tag="means_then_tok_b2")
         for m in range(TOKEN_TILES):
@@ -255,7 +248,7 @@ def tile_shiftedpatchtokenization_pb_kernel(tc, x, ln2_g, ln2_b, w2_words, w2_sc
                         start = first + 64 * dj + 8 * di
                         nc.tensor.transpose(
                             out=quarters[:, :, qx, :, right, :], in_=cells[:, py, px, start : start + P],
-                            identity=sort_ch[:],
+                            identity=ident[:],
                         )
                 if di != 0:
                     scale_and_shift(

@@ -24,7 +24,7 @@ PAD = 72
 PLANE = PAD + TOKENS + PAD
 EPS_36 = 36.0 * 1e-5
 FIRST_TILES = 2
-SQUARES_ON_SCALAR = (16, 10)
+SQUARES_ON_SCALAR = (16, 12)
 VECTOR_COLS = 16
 HALF = P // 2
 
@@ -83,6 +83,9 @@ def tile_shiftedpatchtokenization_pb_kernel(tc, x, ln2_g, ln2_b, w2_words, w2_sc
         at_edge = keep.tile([P, 2], F32)
         inside = keep.tile([P, 2], F32)
         squares = keep.tile([P, 2, 16, 64], F32)
+        pair_sums = keep.tile([P, 16, 2, 16], F32)
+        gain = keep.tile([P, PASSES, PACK], F32)
+        offs = keep.tile([P, PASSES, PACK], F32)
         by_e = []
         for th in range(2):
             by_e.append(x_sb[:, th].rearrange("p e (h y ry c rx) -> p h y ry c rx e", h=2, y=2, ry=2, c=64, rx=2))
@@ -147,8 +150,13 @@ def tile_shiftedpatchtokenization_pb_kernel(tc, x, ln2_g, ln2_b, w2_words, w2_sc
                         in1=banks[unit][:].rearrange("p (e y X xx) -> p y X xx e", e=4, y=2, xx=4),
                         op=ALU.add,
                     )
+                if th == 0:
+                    nc.gpsimd.tensor_tensor(out=pair_sums[:], in0=hw[:, 1:17, 0, 0:2, :], in1=hw[:, 1:17, 0, 2:4, :], op=ALU.add)
+            nc.gpsimd.tensor_copy(out=gain[:], in_=gain_bf[:])
+            nc.gpsimd.tensor_copy(out=offs[:], in_=offs_bf[:])
+            for th in range(2):
                 cell_values = hw[:, 1:17, th].rearrange("p X yy r -> p X (yy r)")
-                nc.vector.tensor_reduce(out=parts[:, 0, th, 1:17], in_=cell_values, axis=AXIS.X, op=ALU.add)
+                nc.vector.tensor_reduce(out=parts[:, 0, th, 1:17], in_=cell_values if th else pair_sums[:].rearrange("p X yy r -> p X (yy r)"), axis=AXIS.X, op=ALU.add)
                 for X in range(16):
                     square_sum = parts[:, 1, th, 1 + X : 2 + X]
                     if X < SQUARES_ON_SCALAR[th]:
@@ -181,8 +189,8 @@ def tile_shiftedpatchtokenization_pb_kernel(tc, x, ln2_g, ln2_b, w2_words, w2_sc
                 else:
                     nc.vector.tensor_copy(out=to, in_=by_py)
 
-            empty_cell_bank(0, 0, True)
             empty_cell_bank(0, 1, True)
+            empty_cell_bank(1, 0, True)
             row_sums = keep.tile([P, 2, 2, 2, 8], F32)
             ends = parts[:].rearrange("p s th (J two) -> p s th J two", two=2)
             nc.vector.tensor_tensor(
@@ -199,7 +207,7 @@ def tile_shiftedpatchtokenization_pb_kernel(tc, x, ln2_g, ln2_b, w2_words, w2_sc
                     rhs=row_sums[:, kind].rearrange("p s th j -> p (s th j)"),
                     start=(kind == OUTER), stop=(kind == OWN),
                 )
-            empty_cell_bank(1, 0, False)
+            empty_cell_bank(0, 0, False)
             means = keep.tile([P, 2, TOKEN_TILES], F32, tag="means_then_tok_b2")
             mean = means[:, 0, :]
             spread = keep.tile([P, TOKEN_TILES], F32)
@@ -231,52 +239,57 @@ def tile_shiftedpatchtokenization_pb_kernel(tc, x, ln2_g, ln2_b, w2_words, w2_sc
         for m in range(TOKEN_TILES):
             y_m = keep.tile([P, 2, 64, 20], F32, name="y%d" % m)
             y.append(y_m)
+
+        turns = []
+        for pair in range(2):
+            for oy in (0, 1, -1):
+                turns.append((2 * pair, oy))
+                turns.append((2 * pair + 1, oy))
+        for m in range(TOKEN_TILES):
+            turns.append((m, 2))
+        for m, oy in turns:
+            y_m = y[m]
             first = PAD + P * m
-            for oy in (0, 1, -1, 2):
-                down = (oy + 1) // 2
-                qy = oy + 1 - 2 * down
-                py, di = oy % 2, oy // 2
-                bank = psum.tile([P, 512], F32, tag="bank")
-                if di == 0:
-                    quarters = bank[:].rearrange("p (a right qx xx e) -> p a qx xx right e", a=8, right=2, qx=2, xx=4)
-                else:
-                    quarters = bank[:].rearrange("p (a qx xx right e) -> p a qx xx right e", a=8, qx=2, xx=4, right=2)
-                for qx in range(2):
-                    for right in range(2):
-                        ox = qx - 1 + 2 * right
-                        px, dj = ox % 2, ox // 2
-                        start = first + 64 * dj + 8 * di
-                        nc.tensor.transpose(
-                            out=quarters[:, :, qx, :, right, :], in_=cells[:, py, px, start : start + P],
-                            identity=ident[:],
-                        )
-                if di != 0:
-                    scale_and_shift(
-                        nc, m, y_m[:, :, 32 * qy : 32 * qy + 32, 4 + 8 * down : 12 + 8 * down],
-                        bank[:].rearrange("p (th pix e) -> p th pix e", th=2, e=8),
-                        rstd[:, {-1: 1, 1: 2}[di], m : m + 1], shift[:, m : m + 1],
-                    )
-                    continue
-                by_right = bank[:].rearrange("p (th yy right q e) -> p right th yy q e", th=2, yy=4, right=2, q=8, e=4)
+            down = (oy + 1) // 2
+            qy = oy + 1 - 2 * down
+            py, di = oy % 2, oy // 2
+            bank = psum.tile([P, 512], F32, tag="bank")
+            if di == 0:
+                quarters = bank[:].rearrange("p (a right qx xx e) -> p a qx xx right e", a=8, right=2, qx=2, xx=4)
+            else:
+                quarters = bank[:].rearrange("p (a qx xx right e) -> p a qx xx right e", a=8, qx=2, xx=4, right=2)
+            for qx in range(2):
                 for right in range(2):
-                    s = 1 + 2 * down + right
-                    scale_and_shift(
-                        nc, m,
-                        y_m[:, :, 32 * qy : 32 * qy + 32, 4 * s : 4 * s + 4].rearrange("p th (yy q) e -> p th yy q e", yy=4),
-                        by_right[:, right], rstd[:, 0, m : m + 1], shift[:, m : m + 1],
+                    ox = qx - 1 + 2 * right
+                    px, dj = ox % 2, ox // 2
+                    start = first + 64 * dj + 8 * di
+                    nc.tensor.transpose(
+                        out=quarters[:, :, qx, :, right, :], in_=cells[:, py, px, start : start + P],
+                        identity=ident[:],
                     )
-                middle = bank[:].rearrange("p (th yy c) -> p th yy c", th=2, yy=4)[:, :, :, 16:48]
+            if di != 0:
+                scale_and_shift(
+                    nc, m, y_m[:, :, 32 * qy : 32 * qy + 32, 4 + 8 * down : 12 + 8 * down],
+                    bank[:].rearrange("p (th pix e) -> p th pix e", th=2, e=8),
+                    rstd[:, {-1: 1, 1: 2}[di], m : m + 1], shift[:, m : m + 1],
+                )
+                continue
+            by_right = bank[:].rearrange("p (th yy right q e) -> p right th yy q e", th=2, yy=4, right=2, q=8, e=4)
+            for right in range(2):
+                s = 1 + 2 * down + right
                 scale_and_shift(
                     nc, m,
-                    y_m[:, :, 32 * oy : 32 * oy + 32, 0:4].rearrange("p th (yy q) e -> p th yy q e", yy=4),
-                    middle.rearrange("p th yy (q e) -> p th yy q e", e=4),
-                    rstd[:, 0, m : m + 1], shift[:, m : m + 1],
+                    y_m[:, :, 32 * qy : 32 * qy + 32, 4 * s : 4 * s + 4].rearrange("p th (yy q) e -> p th yy q e", yy=4),
+                    by_right[:, right], rstd[:, 0, m : m + 1], shift[:, m : m + 1],
                 )
+            middle = bank[:].rearrange("p (th yy c) -> p th yy c", th=2, yy=4)[:, :, :, 16:48]
+            scale_and_shift(
+                nc, m,
+                y_m[:, :, 32 * oy : 32 * oy + 32, 0:4].rearrange("p th (yy q) e -> p th yy q e", yy=4),
+                middle.rearrange("p th yy (q e) -> p th yy q e", e=4),
+                rstd[:, 0, m : m + 1], shift[:, m : m + 1],
+            )
 
-        gain = keep.tile([P, PASSES, PACK], F32)
-        offs = keep.tile([P, PASSES, PACK], F32)
-        nc.gpsimd.tensor_copy(out=gain[:], in_=gain_bf[:])
-        nc.gpsimd.tensor_copy(out=offs[:], in_=offs_bf[:])
         z_words = keep.tile([P, PASSES, TOKENS], U32, align_bytes=64)
         z_scales = keep.tile([P, PASSES, TOKENS], U8, align_bytes=64)
         def quantise(g, z_grouped):
@@ -328,7 +341,7 @@ def tile_shiftedpatchtokenization_pb_kernel(tc, x, ln2_g, ln2_b, w2_words, w2_sc
 
         def finish(acc, m, cut):
             lo, hi = cut
-            result = work.tile([P, 512], F32, bufs=4)
+            result = work.tile([P, 512], F32, bufs=8)
             nc.vector.tensor_tensor(
                 out=result[:, 0 : hi - lo], in0=acc[:, 0 : hi - lo], in1=tok_b2[:, m, lo:hi], op=ALU.add
             )

@@ -20,10 +20,11 @@ PACK = 4
 PASSES = K // (P * PACK)
 DIM = 768
 N_CUTS = ((0, 512), (512, 768))
+LAST_CUTS = ((0, 512), (512, 640), (640, 768))
 PAD = 72
 PLANE = PAD + TOKENS + PAD
 EPS_36 = 36.0 * 1e-5
-FIRST_TILES = 2
+VECTOR_BANKS = ((1, 1), (3, 4))
 SQUARES_ON_SCALAR = (16, 12)
 VECTOR_COLS = 16
 HALF = P // 2
@@ -292,11 +293,21 @@ def tile_shiftedpatchtokenization_pb_kernel(tc, x, ln2_g, ln2_b, w2_words, w2_sc
 
         z_words = keep.tile([P, PASSES, TOKENS], U32, align_bytes=64)
         z_scales = keep.tile([P, PASSES, TOKENS], U8, align_bytes=64)
-        def quantise(g, z_grouped):
-            nc.vector.quantize_mx(
-                out=z_words[:, g, :].bitcast(FP8X4), scales=z_scales[:, g, :],
-                in_=z_grouped[:].rearrange("p n t -> p (n t)"),
+        def group(z_planes, tokens):
+            z_grouped = work.tile([P, TOKENS, PACK], BF16, align_bytes=64, bufs=3)
+            nc.vector.tensor_copy(
+                out=z_grouped[:, tokens].rearrange("p (c i) t -> p c t i", i=4),
+                in_=z_planes[:, :, tokens].rearrange("p t (c i) -> p c t i", i=4),
             )
+            return z_grouped
+
+        def quantise(g, z_grouped, tokens):
+            nc.vector.quantize_mx(
+                out=z_words[:, g, tokens].bitcast(FP8X4), scales=z_scales[:, g, tokens],
+                in_=z_grouped[:, tokens].rearrange("p n t -> p (n t)"),
+            )
+
+        ALL, FIRST_HALF, SECOND_HALF = slice(0, TOKENS), slice(0, TOKENS // 2), slice(TOKENS // 2, TOKENS)
 
         with tc.manual_schedule(engines={mybir.EngineType.DVE}):
             waiting = []
@@ -312,19 +323,21 @@ def tile_shiftedpatchtokenization_pb_kernel(tc, x, ln2_g, ln2_b, w2_words, w2_sc
                             identity=ident[:],
                         )
                     scale_and_shift(
-                        nc, 1 if (t == 1 and g % 2 == 0) else 0, z_planes[:, t, :].rearrange("p (b i j) -> p b i j", b=8, i=8),
+                        nc, 1 if (t, g) in VECTOR_BANKS else 0, z_planes[:, t, :].rearrange("p (b i j) -> p b i j", b=8, i=8),
                         bank[:].rearrange("p (j i b) -> p b i j", j=8, i=8),
                         gain[:, g, t : t + 1], offs[:, g, t : t + 1],
                     )
-                    if t == 1 and waiting:
-                        quantise(g - 1, waiting.pop())
-                z_grouped = work.tile([P, TOKENS, PACK], BF16, align_bytes=64)
-                nc.vector.tensor_copy(
-                    out=z_grouped[:].rearrange("p (c i) t -> p c t i", i=4),
-                    in_=z_planes[:].rearrange("p t (c i) -> p c t i", i=4),
-                )
-                waiting.append(z_grouped)
-            quantise(PASSES - 1, waiting.pop())
+                if g < PASSES - 1:
+                    z_grouped = group(z_planes, ALL)
+                    if waiting:
+                        quantise(g - 1, waiting.pop(), ALL)
+                    waiting.append(z_grouped)
+            halves = []
+            for tokens in (FIRST_HALF, SECOND_HALF):
+                halves.append((PASSES - 1, group(z_planes, tokens), tokens))
+            quantise(PASSES - 2, waiting.pop(), ALL)
+            for half in halves:
+                quantise(*half)
 
         out_rows = out.flatten_outer_dims()
 
@@ -347,17 +360,22 @@ def tile_shiftedpatchtokenization_pb_kernel(tc, x, ln2_g, ln2_b, w2_words, w2_sc
             )
             nc.sync.dma_start(out=out_rows[P * m : P * m + P, lo:hi], in_=result[:, 0 : hi - lo])
 
-        first_groups = []
-        for m in range(FIRST_TILES):
-            for cut in N_CUTS:
+        cuts = []
+        for m in range(TOKEN_TILES):
+            for cut in N_CUTS if m < TOKEN_TILES - 1 else LAST_CUTS:
+                cuts.append((m, cut))
+        with tc.manual_schedule(engines={mybir.EngineType.PE}):
+            first_groups = []
+            for m, cut in cuts[0:5]:
                 acc = psum.tile([P, 512], F32, tag="bank")
-                mx_passes(acc, m, cut, range(PASSES - 1))
                 first_groups.append((acc, m, cut))
-        for acc, m, cut in first_groups:
-            mx_passes(acc, m, cut, (PASSES - 1,))
-            finish(acc, m, cut)
-        for m in range(FIRST_TILES, TOKEN_TILES):
-            for cut in N_CUTS:
+            for passes in (0, 1, 2, 3):
+                for acc, m, cut in first_groups:
+                    mx_passes(acc, m, cut, (passes,))
+            for acc, m, cut in first_groups:
+                mx_passes(acc, m, cut, (PASSES - 1,))
+                finish(acc, m, cut)
+            for m, cut in cuts[5:]:
                 acc = psum.tile([P, 512], F32, tag="bank")
                 mx_passes(acc, m, cut, range(PASSES))
                 finish(acc, m, cut)

@@ -24,7 +24,8 @@ LAST_CUTS = ((0, 512), (512, 640), (640, 768))
 PAD = 72
 PLANE = PAD + TOKENS + PAD
 EPS_36 = 36.0 * 1e-5
-VECTOR_BANKS = ((1, 1), (3, 4))
+FIRST_GROUPS = 4
+VECTOR_BANKS = ((1, 1), (1, 3), (3, 4))
 SQUARES_ON_SCALAR = (16, 12)
 VECTOR_COLS = 16
 HALF = P // 2
@@ -241,19 +242,9 @@ def tile_shiftedpatchtokenization_pb_kernel(tc, x, ln2_g, ln2_b, w2_words, w2_sc
             y_m = keep.tile([P, 2, 64, 20], F32, name="y%d" % m)
             y.append(y_m)
 
-        turns = []
-        for pair in range(2):
-            for oy in (0, 1, -1):
-                turns.append((2 * pair, oy))
-                turns.append((2 * pair + 1, oy))
-        for m in range(TOKEN_TILES):
-            turns.append((m, 2))
-        for m, oy in turns:
-            y_m = y[m]
-            first = PAD + P * m
-            down = (oy + 1) // 2
-            qy = oy + 1 - 2 * down
+        def cell_row(m, oy):
             py, di = oy % 2, oy // 2
+            first = PAD + P * m
             bank = psum.tile([P, 512], F32, tag="bank")
             if di == 0:
                 quarters = bank[:].rearrange("p (a right qx xx e) -> p a qx xx right e", a=8, right=2, qx=2, xx=4)
@@ -265,31 +256,67 @@ def tile_shiftedpatchtokenization_pb_kernel(tc, x, ln2_g, ln2_b, w2_words, w2_sc
                     px, dj = ox % 2, ox // 2
                     start = first + 64 * dj + 8 * di
                     nc.tensor.transpose(
-                        out=quarters[:, :, qx, :, right, :], in_=cells[:, py, px, start : start + P],
-                        identity=ident[:],
+                        out=quarters[:, :, qx, :, right, :], in_=cells[:, py, px, start : start + P], identity=ident[:]
                     )
-            if di != 0:
-                scale_and_shift(
-                    nc, m, y_m[:, :, 32 * qy : 32 * qy + 32, 4 + 8 * down : 12 + 8 * down],
-                    bank[:].rearrange("p (th pix e) -> p th pix e", th=2, e=8),
-                    rstd[:, {-1: 1, 1: 2}[di], m : m + 1], shift[:, m : m + 1],
-                )
-                continue
+            return bank
+
+        def empty_outer(m, oy, bank):
+            down = (oy + 1) // 2
+            qy = oy + 1 - 2 * down
+            scale_and_shift(
+                nc, m, y[m][:, :, 32 * qy : 32 * qy + 32, 4 + 8 * down : 12 + 8 * down],
+                bank[:].rearrange("p (th pix e) -> p th pix e", th=2, e=8),
+                rstd[:, {-1: 1, 2: 2}[oy], m : m + 1], shift[:, m : m + 1],
+            )
+
+        def empty_shifted(m, oy, bank):
+            down = (oy + 1) // 2
+            qy = oy + 1 - 2 * down
             by_right = bank[:].rearrange("p (th yy right q e) -> p right th yy q e", th=2, yy=4, right=2, q=8, e=4)
             for right in range(2):
                 s = 1 + 2 * down + right
                 scale_and_shift(
                     nc, m,
-                    y_m[:, :, 32 * qy : 32 * qy + 32, 4 * s : 4 * s + 4].rearrange("p th (yy q) e -> p th yy q e", yy=4),
+                    y[m][:, :, 32 * qy : 32 * qy + 32, 4 * s : 4 * s + 4].rearrange("p th (yy q) e -> p th yy q e", yy=4),
                     by_right[:, right], rstd[:, 0, m : m + 1], shift[:, m : m + 1],
                 )
+
+        def empty_unshifted(m, oy, bank):
             middle = bank[:].rearrange("p (th yy c) -> p th yy c", th=2, yy=4)[:, :, :, 16:48]
             scale_and_shift(
                 nc, m,
-                y_m[:, :, 32 * oy : 32 * oy + 32, 0:4].rearrange("p th (yy q) e -> p th yy q e", yy=4),
+                y[m][:, :, 32 * oy : 32 * oy + 32, 0:4].rearrange("p th (yy q) e -> p th yy q e", yy=4),
                 middle.rearrange("p th yy (q e) -> p th yy q e", e=4),
                 rstd[:, 0, m : m + 1], shift[:, m : m + 1],
             )
+
+        for pair in ((0, 1), (2, 3)):
+            for m in pair:
+                bank = cell_row(m, 1)
+                empty_shifted(m, 1, bank)
+                empty_unshifted(m, 1, bank)
+            for m in pair:
+                empty_outer(m, -1, cell_row(m, -1))
+        upper_middle = []
+        for m in range(TOKEN_TILES):
+            bank = cell_row(m, 0)
+            empty_unshifted(m, 0, bank)
+            upper_middle.append(bank)
+
+        lowest = []
+        for m in (0, 1):
+            bank = cell_row(m, 2)
+            lowest.append(bank)
+
+        def rest_of_step_5(part):
+            if part == 0:
+                for m in range(TOKEN_TILES):
+                    empty_shifted(m, 0, upper_middle[m])
+                for m in (0, 1):
+                    empty_outer(m, 2, lowest[m])
+            else:
+                for m in (2, 3):
+                    empty_outer(m, 2, cell_row(m, 2))
 
         z_words = keep.tile([P, PASSES, TOKENS], U32, align_bytes=64)
         z_scales = keep.tile([P, PASSES, TOKENS], U8, align_bytes=64)
@@ -313,29 +340,32 @@ def tile_shiftedpatchtokenization_pb_kernel(tc, x, ln2_g, ln2_b, w2_words, w2_sc
             waiting = []
             for g in range(PASSES):
                 z_planes = work.tile([P, PACK, TOKENS], BF16)
+                banks = []
                 for t in range(PACK):
                     th, tl = t // 2, t % 2
                     bank = psum.tile([P, 512], F32, tag="bank")
+                    banks.append(bank)
                     for m in range(TOKEN_TILES):
                         half = y[m][:, th].rearrange("p pix e -> p (pix e)")
                         nc.tensor.transpose(
                             out=bank[:, P * m : P * m + P], in_=half[:, 256 * g + tl : 256 * g + 256 : 2],
                             identity=ident[:],
                         )
+                    if g == 0 and t < 2:
+                        rest_of_step_5(t)
+                for t in range(PACK):
                     scale_and_shift(
                         nc, 1 if (t, g) in VECTOR_BANKS else 0, z_planes[:, t, :].rearrange("p (b i j) -> p b i j", b=8, i=8),
-                        bank[:].rearrange("p (j i b) -> p b i j", j=8, i=8),
+                        banks[t][:].rearrange("p (j i b) -> p b i j", j=8, i=8),
                         gain[:, g, t : t + 1], offs[:, g, t : t + 1],
                     )
+                if waiting:
+                    quantise(g - 1, waiting.pop(), ALL)
                 if g < PASSES - 1:
-                    z_grouped = group(z_planes, ALL)
-                    if waiting:
-                        quantise(g - 1, waiting.pop(), ALL)
-                    waiting.append(z_grouped)
+                    waiting.append(group(z_planes, ALL))
             halves = []
             for tokens in (FIRST_HALF, SECOND_HALF):
                 halves.append((PASSES - 1, group(z_planes, tokens), tokens))
-            quantise(PASSES - 2, waiting.pop(), ALL)
             for half in halves:
                 quantise(*half)
 
@@ -364,18 +394,15 @@ def tile_shiftedpatchtokenization_pb_kernel(tc, x, ln2_g, ln2_b, w2_words, w2_sc
         for m in range(TOKEN_TILES):
             for cut in N_CUTS if m < TOKEN_TILES - 1 else LAST_CUTS:
                 cuts.append((m, cut))
-        with tc.manual_schedule(engines={mybir.EngineType.PE}):
-            first_groups = []
-            for m, cut in cuts[0:5]:
-                acc = psum.tile([P, 512], F32, tag="bank")
-                first_groups.append((acc, m, cut))
-            for passes in (0, 1, 2, 3):
-                for acc, m, cut in first_groups:
-                    mx_passes(acc, m, cut, (passes,))
-            for acc, m, cut in first_groups:
-                mx_passes(acc, m, cut, (PASSES - 1,))
-                finish(acc, m, cut)
-            for m, cut in cuts[5:]:
-                acc = psum.tile([P, 512], F32, tag="bank")
-                mx_passes(acc, m, cut, range(PASSES))
-                finish(acc, m, cut)
+        first_groups = []
+        for m, cut in cuts[0:FIRST_GROUPS]:
+            acc = psum.tile([P, 512], F32, tag="bank")
+            mx_passes(acc, m, cut, range(PASSES - 1))
+            first_groups.append((acc, m, cut))
+        for acc, m, cut in first_groups:
+            mx_passes(acc, m, cut, (PASSES - 1,))
+            finish(acc, m, cut)
+        for m, cut in cuts[FIRST_GROUPS:]:
+            acc = psum.tile([P, 512], F32, tag="bank")
+            mx_passes(acc, m, cut, range(PASSES))
+            finish(acc, m, cut)

import concourse.mybir as mybir
from concourse.masks import make_identity

F32 = mybir.dt.float32
BF16 = mybir.dt.bfloat16
I32 = mybir.dt.int32
U32 = mybir.dt.uint32
U8 = mybir.dt.uint8
FP8X4 = mybir.dt.float8_e4m3fn_x4
ALU = mybir.AluOpType
ACT = mybir.ActivationFunctionType
AXIS = mybir.AxisListType

P = 128
CHANNELS = 8
TOKENS = 512
TOKEN_TILES = TOKENS // P
K = 2560
PACK = 4
PASSES = K // (P * PACK)
DIM = 768
N_CUTS = ((0, 512), (512, 768))
LAST_CUTS = ((0, 512), (512, 640), (640, 768))
PAD = 72
PLANE = PAD + TOKENS + PAD
EPS_36 = 36.0 * 1e-5
FIRST_GROUPS = 4
VECTOR_BANKS = ((1, 1), (1, 3), (3, 4))
SQUARES_ON_SCALAR = (16, 12)
VECTOR_COLS = 16
HALF = P // 2

FLOPS = 2 * TOKENS * K * DIM


def scale_and_shift(nc, m, out, in_, scale, shift):
    if m % 2 == 0:
        nc.scalar.activation(out=out, in_=in_, func=ACT.Identity, bias=shift, scale=scale)
    else:
        nc.vector.tensor_scalar(out=out, in0=in_, scalar1=scale, scalar2=shift, op0=ALU.mult, op1=ALU.add)


def tile_shiftedpatchtokenization_pb_kernel(tc, x, ln2_g, ln2_b, w2_words, w2_scales, b2, tok, out):
    nc = tc.nc
    with tc.tile_pool(name="keep", bufs=1) as keep, tc.tile_pool(name="work", bufs=2) as work, tc.psum_pool(
        name="psum", bufs=8
    ) as psum:
        x_sb = keep.tile([P, 2, 4, 1024], BF16)
        for th in range(2):
            for e in range(4):
                channel = 4 * (e // 2) + 2 * th + e % 2
                nc.sync.dma_start(out=x_sb[:, th, e, :], in_=x[:, channel].rearrange("b (iy r) w -> iy b (r w)", r=8))

        tok_bf = keep.tile([P, TOKEN_TILES, DIM], BF16)
        nc.sync.dma_start(out=tok_bf[:], in_=tok.flatten_outer_dims().rearrange("(m p) n -> p m n", p=P))
        b2_bf = keep.tile([P, DIM], BF16)
        nc.sync.dma_start(out=b2_bf[:], in_=b2.partition_broadcast(P))

        gain_bf = keep.tile([P, PASSES, PACK], BF16)
        offs_bf = keep.tile([P, PASSES, PACK], BF16)
        nc.sync.dma_start(out=gain_bf[:], in_=ln2_g.rearrange("(g p t) -> p g t", g=PASSES, p=P))
        nc.sync.dma_start(out=offs_bf[:], in_=ln2_b.rearrange("(g p t) -> p g t", g=PASSES, p=P))

        w_scales = keep.tile([P, PASSES, DIM], U8, align_bytes=64)
        nc.vector.memset(w_scales[:].bitcast(I32), 0)
        for quad in range(4):
            nc.sync.dma_start(
                out=w_scales[32 * quad : 32 * quad + 4].bitcast(I32),
                in_=w2_scales[:, 4 * quad : 4 * quad + 4, :].rearrange("g r n -> r g n").bitcast(I32),
            )
        w_words = keep.tile([P, PASSES, DIM], U32, align_bytes=64)
        nc.sync.dma_start(
            out=w_words[:].bitcast(I32), in_=w2_words.rearrange("g p n t -> p g (n t)").bitcast(I32)
        )

        OUTER, OWN = 0, 1
        pick_rows = keep.tile([P, 2, 2, 8, 8], F32)
        one = keep.tile([P, 1], F32)
        ident = keep.tile([P, P], F32)
        ident_k = keep.tile([P, P], F32)
        neg_ident = keep.tile([P, P], BF16)
        hw = keep.tile([P, 18, 2, 4, 16], F32)
        parts = keep.tile([P, 2, 2, 18], F32)
        cells = keep.tile([P, 2, 2, PLANE], F32)
        at_edge = keep.tile([P, 2], F32)
        inside = keep.tile([P, 2], F32)
        squares = keep.tile([P, 2, 16, 64], F32)
        pair_sums = keep.tile([P, 16, 2, 16], F32)
        gain = keep.tile([P, PASSES, PACK], F32)
        offs = keep.tile([P, PASSES, PACK], F32)
        by_e = []
        for th in range(2):
            by_e.append(x_sb[:, th].rearrange("p e (h y ry c rx) -> p h y ry c rx e", h=2, y=2, ry=2, c=64, rx=2))

        with tc.manual_schedule(engines={mybir.EngineType.DVE, mybir.EngineType.Pool}):
            nc.vector.memset(one[:], 1.0)
            nc.scalar.activation(out=one[:], in_=one[:], func=ACT.Abs_reciprocal_sqrt)
            make_identity(nc, ident[:])
            nc.vector.memset(parts[:], 0.0)
            nc.vector.memset(hw[:, 0], 0.0)
            nc.vector.memset(hw[:, 17], 0.0)
            nc.vector.tensor_scalar(out=neg_ident[:], in0=ident[:], scalar1=-1.0, scalar2=None, op0=ALU.mult)
            nc.vector.tensor_scalar(out=ident_k[:], in0=ident[:], scalar1=1.0 / K, scalar2=None, op0=ALU.mult)
            by_row = ident_k[:].rearrange("p (i q b) -> p q i b", i=8, q=2, b=8)
            outer = pick_rows[:, OUTER, 0]
            own = pick_rows[:, OWN, 0]
            nc.vector.tensor_tensor(out=own, in0=by_row[:, 0], in1=by_row[:, 1], op=ALU.add)
            nc.vector.tensor_copy(out=outer, in_=own)
            nc.vector.tensor_tensor(out=outer[:, 1:8], in0=outer[:, 1:8], in1=by_row[:, 1, 0:7], op=ALU.add)
            nc.vector.tensor_tensor(out=outer[:, 0:7], in0=outer[:, 0:7], in1=by_row[:, 0, 1:8], op=ALU.add)
            nc.vector.tensor_tensor(out=own, in0=own, in1=outer, op=ALU.add)
            nc.vector.tensor_copy(out=pick_rows[:, OUTER, 1], in_=outer)
            nc.vector.tensor_copy(out=pick_rows[:, OWN, 1], in_=own)

            nc.vector.memset(cells[:, :, :, 0:PAD], 0.0)
            nc.vector.memset(cells[:, :, :, PAD + TOKENS : PLANE], 0.0)
            by_token = ident[:].rearrange("p (jlo i b) -> p jlo i b", jlo=2, i=8, b=8)
            nc.vector.tensor_reduce(out=at_edge[:, 0:1], in_=by_token[:, :, 0, :], axis=AXIS.XY, op=ALU.add)
            nc.vector.tensor_reduce(out=at_edge[:, 1:2], in_=by_token[:, :, 7, :], axis=AXIS.XY, op=ALU.add)
            nc.vector.tensor_scalar(out=inside[:], in0=at_edge[:], scalar1=-1.0, scalar2=1.0, op0=ALU.mult, op1=ALU.add)

            banks = []
            uppers = []
            for th in range(2):
                for yyh in range(2):
                    minus = psum.tile([P, 512], F32, tag="bank")
                    banks.append(minus)
                for e in range(4):
                    blocks = x_sb[:, th, e].rearrange("p (h y ry c rx) -> p h y ry c rx", h=2, y=2, ry=2, c=64, rx=2)
                    for yyh in range(2):
                        unit = 2 * th + yyh
                        cols = banks[unit][:, P * e : P * e + P].rearrange("p (y c) -> p y c", y=2)
                        for n, (ry, rx) in enumerate(((1, 0), (0, 1), (1, 1))):
                            skip = VECTOR_COLS if (unit, ry, rx) == (0, 0, 1) else 0
                            nc.tensor.matmul(
                                out=cols[:, :, skip:], lhsT=neg_ident[:], rhs=blocks[:, yyh, :, ry, skip:, rx],
                                start=(n == 0), stop=(n == 2),
                            )
                for yyh in range(2):
                    upper = work.tile([P, 2, 64, 4], F32, bufs=4)
                    uppers.append(upper)
                    nc.scalar.activation(out=upper[:], in_=by_e[th][:, yyh, :, 0, :, 0, :], func=ACT.Copy, scale=3.0)
            few = uppers[0][:, :, 0:VECTOR_COLS, :]
            nc.vector.tensor_tensor(out=few, in0=few, in1=by_e[0][:, 0, :, 0, 0:VECTOR_COLS, 1, :], op=ALU.subtract)
            for th in range(2):
                for yyh in range(2):
                    unit = 2 * th + yyh
                    hw_unit = hw[:, 1:17, th, 2 * yyh : 2 * yyh + 2, :]
                    nc.vector.tensor_tensor(
                        out=hw_unit.rearrange("p X y (xx e) -> p y X xx e", xx=4),
                        in0=uppers[unit][:].rearrange("p y (X xx) e -> p y X xx e", xx=4),
                        in1=banks[unit][:].rearrange("p (e y X xx) -> p y X xx e", e=4, y=2, xx=4),
                        op=ALU.add,
                    )
                if th == 0:
                    nc.gpsimd.tensor_tensor(out=pair_sums[:], in0=hw[:, 1:17, 0, 0:2, :], in1=hw[:, 1:17, 0, 2:4, :], op=ALU.add)
            nc.gpsimd.tensor_copy(out=gain[:], in_=gain_bf[:])
            nc.gpsimd.tensor_copy(out=offs[:], in_=offs_bf[:])
            for th in range(2):
                cell_values = hw[:, 1:17, th].rearrange("p X yy r -> p X (yy r)")
                nc.vector.tensor_reduce(out=parts[:, 0, th, 1:17], in_=cell_values if th else pair_sums[:].rearrange("p X yy r -> p X (yy r)"), axis=AXIS.X, op=ALU.add)
                for X in range(16):
                    square_sum = parts[:, 1, th, 1 + X : 2 + X]
                    if X < SQUARES_ON_SCALAR[th]:
                        nc.scalar.activation(
                            out=squares[:, th, X, :], in_=cell_values[:, X, :], func=ACT.Square, accum_out=square_sum
                        )
                    else:
                        nc.vector.scalar_tensor_tensor(
                            out=squares[:, th, X, :], in0=cell_values[:, X, :], scalar=1.0, in1=cell_values[:, X, :],
                            op0=ALU.mult, op1=ALU.mult, accum_out=square_sum,
                        )

            cell_banks = []
            for jh in range(2):
                for px in range(2):
                    bank = psum.tile([P, 512], F32, tag="bank")
                    for jl in range(4):
                        nc.tensor.transpose(
                            out=bank[:, P * jl : P * jl + P],
                            in_=hw[:, 1 + 2 * (4 * jh + jl) + px].rearrange("p th yy r -> p (th yy r)"),
                            identity=ident[:],
                        )
                    cell_banks.append(bank)

            def empty_cell_bank(jh, px, on_scalar):
                by_py = cell_banks[2 * jh + px][:].rearrange("p (ji py b) -> p py ji b", ji=32, py=2, b=8)
                to = cells[:, :, px, PAD + 256 * jh : PAD + 256 * jh + 256].rearrange("p py (ji b) -> p py ji b", b=8)
                if on_scalar:
                    nc.scalar.copy(out=to, in_=by_py)
                else:
                    nc.vector.tensor_copy(out=to, in_=by_py)

            empty_cell_bank(0, 1, True)
            empty_cell_bank(1, 0, True)
            row_sums = keep.tile([P, 2, 2, 2, 8], F32)
            ends = parts[:].rearrange("p s th (J two) -> p s th J two", two=2)
            nc.vector.tensor_tensor(
                out=row_sums[:, OUTER], in0=ends[:, :, :, 0:8, 0], in1=ends[:, :, :, 1:9, 1], op=ALU.add
            )
            nc.vector.tensor_tensor(
                out=row_sums[:, OWN], in0=ends[:, :, :, 0:8, 1], in1=ends[:, :, :, 1:9, 0], op=ALU.add
            )
            totals = psum.tile([P, 512], F32, tag="bank")
            for kind in (OUTER, OWN):
                nc.tensor.matmul(
                    out=totals[:, 0:32],
                    lhsT=pick_rows[:, kind].rearrange("p jlo i b -> p (jlo i b)"),
                    rhs=row_sums[:, kind].rearrange("p s th j -> p (s th j)"),
                    start=(kind == OUTER), stop=(kind == OWN),
                )
            empty_cell_bank(0, 0, False)
            means = keep.tile([P, 2, TOKEN_TILES], F32, tag="means_then_tok_b2")
            mean = means[:, 0, :]
            spread = keep.tile([P, TOKEN_TILES], F32)
            mean_sq = keep.tile([P, TOKEN_TILES], F32)
            by_jlo = totals[:, 0:32].rearrange("p (s th m jlo) -> p jlo s m th", s=2, th=2, jlo=2)
            for jlo in range(2):
                rows = slice(HALF * jlo, HALF * jlo + HALF)
                nc.vector.tensor_reduce(out=means[rows], in_=by_jlo[rows, jlo], axis=AXIS.X, op=ALU.add)
            nc.vector.tensor_tensor(out=mean_sq[:], in0=mean, in1=mean, op=ALU.mult)
            nc.vector.tensor_tensor(out=spread[:], in0=means[:, 1, :], in1=mean_sq[:], op=ALU.subtract)
            rstd = keep.tile([P, 3, TOKEN_TILES], F32)
            shift = keep.tile([P, TOKEN_TILES], F32)
            nc.scalar.activation(out=rstd[:, 0, :], in_=spread[:], func=ACT.Abs_reciprocal_sqrt, bias=EPS_36)
            empty_cell_bank(1, 1, True)
            nc.vector.scalar_tensor_tensor(
                out=shift[:], in0=mean, scalar=-1.0, in1=rstd[:, 0, :], op0=ALU.mult, op1=ALU.mult
            )
            for edge in range(2):
                nc.vector.tensor_scalar(
                    out=rstd[:, 1 + edge, :], in0=rstd[:, 0, :], scalar1=inside[:, edge : edge + 1], scalar2=None,
                    op0=ALU.mult,
                )

        tok_b2 = keep.tile([P, TOKEN_TILES, DIM], F32, tag="means_then_tok_b2")
        for m in range(TOKEN_TILES):
            nc.gpsimd.tensor_tensor(out=tok_b2[:, m, :], in0=tok_bf[:, m, :], in1=b2_bf[:], op=ALU.add)

        y = []
        for m in range(TOKEN_TILES):
            y_m = keep.tile([P, 2, 64, 20], F32, name="y%d" % m)
            y.append(y_m)

        def cell_row(m, oy):
            py, di = oy % 2, oy // 2
            first = PAD + P * m
            bank = psum.tile([P, 512], F32, tag="bank")
            if di == 0:
                quarters = bank[:].rearrange("p (a right qx xx e) -> p a qx xx right e", a=8, right=2, qx=2, xx=4)
            else:
                quarters = bank[:].rearrange("p (a qx xx right e) -> p a qx xx right e", a=8, qx=2, xx=4, right=2)
            for qx in range(2):
                for right in range(2):
                    ox = qx - 1 + 2 * right
                    px, dj = ox % 2, ox // 2
                    start = first + 64 * dj + 8 * di
                    nc.tensor.transpose(
                        out=quarters[:, :, qx, :, right, :], in_=cells[:, py, px, start : start + P], identity=ident[:]
                    )
            return bank

        def empty_outer(m, oy, bank):
            down = (oy + 1) // 2
            qy = oy + 1 - 2 * down
            scale_and_shift(
                nc, m, y[m][:, :, 32 * qy : 32 * qy + 32, 4 + 8 * down : 12 + 8 * down],
                bank[:].rearrange("p (th pix e) -> p th pix e", th=2, e=8),
                rstd[:, {-1: 1, 2: 2}[oy], m : m + 1], shift[:, m : m + 1],
            )

        def empty_shifted(m, oy, bank):
            down = (oy + 1) // 2
            qy = oy + 1 - 2 * down
            by_right = bank[:].rearrange("p (th yy right q e) -> p right th yy q e", th=2, yy=4, right=2, q=8, e=4)
            for right in range(2):
                s = 1 + 2 * down + right
                scale_and_shift(
                    nc, m,
                    y[m][:, :, 32 * qy : 32 * qy + 32, 4 * s : 4 * s + 4].rearrange("p th (yy q) e -> p th yy q e", yy=4),
                    by_right[:, right], rstd[:, 0, m : m + 1], shift[:, m : m + 1],
                )

        def empty_unshifted(m, oy, bank):
            middle = bank[:].rearrange("p (th yy c) -> p th yy c", th=2, yy=4)[:, :, :, 16:48]
            scale_and_shift(
                nc, m,
                y[m][:, :, 32 * oy : 32 * oy + 32, 0:4].rearrange("p th (yy q) e -> p th yy q e", yy=4),
                middle.rearrange("p th yy (q e) -> p th yy q e", e=4),
                rstd[:, 0, m : m + 1], shift[:, m : m + 1],
            )

        for pair in ((0, 1), (2, 3)):
            for m in pair:
                bank = cell_row(m, 1)
                empty_shifted(m, 1, bank)
                empty_unshifted(m, 1, bank)
            for m in pair:
                empty_outer(m, -1, cell_row(m, -1))
        upper_middle = []
        for m in range(TOKEN_TILES):
            bank = cell_row(m, 0)
            empty_unshifted(m, 0, bank)
            upper_middle.append(bank)

        lowest = []
        for m in (0, 1):
            bank = cell_row(m, 2)
            lowest.append(bank)

        def rest_of_step_5(part):
            if part == 0:
                for m in range(TOKEN_TILES):
                    empty_shifted(m, 0, upper_middle[m])
                for m in (0, 1):
                    empty_outer(m, 2, lowest[m])
            else:
                for m in (2, 3):
                    empty_outer(m, 2, cell_row(m, 2))

        z_words = keep.tile([P, PASSES, TOKENS], U32, align_bytes=64)
        z_scales = keep.tile([P, PASSES, TOKENS], U8, align_bytes=64)
        def group(z_planes, tokens):
            z_grouped = work.tile([P, TOKENS, PACK], BF16, align_bytes=64, bufs=3)
            nc.vector.tensor_copy(
                out=z_grouped[:, tokens].rearrange("p (c i) t -> p c t i", i=4),
                in_=z_planes[:, :, tokens].rearrange("p t (c i) -> p c t i", i=4),
            )
            return z_grouped

        def quantise(g, z_grouped, tokens):
            nc.vector.quantize_mx(
                out=z_words[:, g, tokens].bitcast(FP8X4), scales=z_scales[:, g, tokens],
                in_=z_grouped[:, tokens].rearrange("p n t -> p (n t)"),
            )

        ALL, FIRST_HALF, SECOND_HALF = slice(0, TOKENS), slice(0, TOKENS // 2), slice(TOKENS // 2, TOKENS)

        with tc.manual_schedule(engines={mybir.EngineType.DVE}):
            waiting = []
            for g in range(PASSES):
                z_planes = work.tile([P, PACK, TOKENS], BF16)
                banks = []
                for t in range(PACK):
                    th, tl = t // 2, t % 2
                    bank = psum.tile([P, 512], F32, tag="bank")
                    banks.append(bank)
                    for m in range(TOKEN_TILES):
                        half = y[m][:, th].rearrange("p pix e -> p (pix e)")
                        nc.tensor.transpose(
                            out=bank[:, P * m : P * m + P], in_=half[:, 256 * g + tl : 256 * g + 256 : 2],
                            identity=ident[:],
                        )
                    if g == 0 and t < 2:
                        rest_of_step_5(t)
                for t in range(PACK):
                    scale_and_shift(
                        nc, 1 if (t, g) in VECTOR_BANKS else 0, z_planes[:, t, :].rearrange("p (b i j) -> p b i j", b=8, i=8),
                        banks[t][:].rearrange("p (j i b) -> p b i j", j=8, i=8),
                        gain[:, g, t : t + 1], offs[:, g, t : t + 1],
                    )
                if waiting:
                    quantise(g - 1, waiting.pop(), ALL)
                if g < PASSES - 1:
                    waiting.append(group(z_planes, ALL))
            halves = []
            for tokens in (FIRST_HALF, SECOND_HALF):
                halves.append((PASSES - 1, group(z_planes, tokens), tokens))
            for half in halves:
                quantise(*half)

        out_rows = out.flatten_outer_dims()

        def mx_passes(acc, m, cut, passes):
            lo, hi = cut
            rows = slice(P * m, P * m + P)
            for g in passes:
                nc.tensor.matmul_mx(
                    out=acc[:, 0 : hi - lo],
                    lhsT=z_words[:, g, rows].bitcast(FP8X4), lhsT_scale=z_scales[:, g, rows],
                    rhs=w_words[:, g, lo:hi].bitcast(FP8X4), rhs_scale=w_scales[:, g, lo:hi],
                    start=(g == 0), stop=(g == PASSES - 1),
                )

        def finish(acc, m, cut):
            lo, hi = cut
            result = work.tile([P, 512], F32, bufs=8)
            nc.vector.tensor_tensor(
                out=result[:, 0 : hi - lo], in0=acc[:, 0 : hi - lo], in1=tok_b2[:, m, lo:hi], op=ALU.add
            )
            nc.sync.dma_start(out=out_rows[P * m : P * m + P, lo:hi], in_=result[:, 0 : hi - lo])

        cuts = []
        for m in range(TOKEN_TILES):
            for cut in N_CUTS if m < TOKEN_TILES - 1 else LAST_CUTS:
                cuts.append((m, cut))
        first_groups = []
        for m, cut in cuts[0:FIRST_GROUPS]:
            acc = psum.tile([P, 512], F32, tag="bank")
            mx_passes(acc, m, cut, range(PASSES - 1))
            first_groups.append((acc, m, cut))
        for acc, m, cut in first_groups:
            mx_passes(acc, m, cut, (PASSES - 1,))
            finish(acc, m, cut)
        for m, cut in cuts[FIRST_GROUPS:]:
            acc = psum.tile([P, 512], F32, tag="bank")
            mx_passes(acc, m, cut, range(PASSES))
            finish(acc, m, cut)
